import numpy as np
import ml_dtypes


def mxq(x, axis, fmt="e4m3"):
    dtype, down = {"e4m3": (ml_dtypes.float8_e4m3fn, 7), "e5m2": (ml_dtypes.float8_e5m2, 14)}[fmt]
    v = np.moveaxis(np.asarray(x, np.float32).astype(ml_dtypes.bfloat16).astype(np.float64), axis, -1)
    blocks = v.reshape(v.shape[:-1] + (-1, 32))
    amax = np.abs(blocks).max(-1, keepdims=True)
    byte = np.maximum(np.where(amax > 0, np.frexp(amax)[1] - 1 + 127, 0) - down, 1)
    scale = np.exp2(byte - 127.0)
    codes = (blocks / scale).astype(np.float32).astype(dtype).astype(np.float64)
    return np.moveaxis((codes * scale).reshape(v.shape), -1, axis)


WIDE = False


def mx_kscale(k):
    if not WIDE:
        return np.ones(k)
    levels = np.array([10, -10, 5, -5, 0])
    if k % 512:
        return np.exp2(np.random.permutation(np.resize(levels, k // 32))).repeat(32)
    a = np.empty((k // 512, 16))
    for p in range(k // 512):
        a[p, :8] = np.random.permutation(np.resize(levels, 8))
        for g in range(8):
            far = levels[np.abs(levels - a[p, g]) >= 10]
            a[p, g + 8] = far[np.random.randint(len(far))]
    return np.exp2(a.ravel()).repeat(32)


BF16 = ml_dtypes.bfloat16


def bf(x):
    return np.asarray(x, np.float32).astype(BF16)


def f64(x):
    return np.asarray(x).astype(np.float64)


B, S, IN, OUT, Q, NS, R, ALPHA = 2, 1024, 2048, 2048, 4, 4, 512, 1024
DO = OUT // Q
SCALING = ALPHA / R


def mix(w, lb):
    b_mix = sum(w[:, :, k, None, None] * lb[None, :, k] for k in range(NS))
    return b_mix.transpose(0, 2, 1, 3).reshape(B, R, OUT)


def setup_inputs():
    s = mx_kscale(S)[None, :, None]
    u = mx_kscale(OUT)
    uq = u.reshape(Q, DO)[:, None, None, :]
    h = bf(np.random.standard_normal((B, S, R)) * s)
    weights = bf(np.random.uniform(0.0, 1.0, (B, Q, NS)))
    lora_b = bf(np.random.standard_normal((Q, NS, R, DO)) / np.sqrt(NS * R) / uq)
    g = bf(np.random.standard_normal((B, S, OUT)) * np.exp2(np.random.randint(-6, 1, (B, S, 1))) / s * u)
    return {"h": h, "weights": weights, "lora_b": lora_b, "grad_out": g}


def reference(h, weights, lora_b, grad_out):
    w, lb, g = f64(weights), f64(lora_b), f64(grad_out)
    b_mix = mix(w, lb)
    dh = (mxq(g, 2, "e5m2") @ mxq(b_mix, 2, "e4m3").transpose(0, 2, 1)) * SCALING
    db = (mxq(f64(h), 1, "e4m3").transpose(0, 2, 1) @ mxq(g, 1, "e5m2")) * SCALING
    db = db.reshape(B, R, Q, DO).transpose(0, 2, 1, 3)
    dlb = sum(w[b, :, :, None, None] * db[b, :, None] for b in range(B))
    return dh, dlb

@@ -1,0 +1,377 @@
+from contextlib import ExitStack
+
+import concourse.mybir as mybir
+from concourse.masks import make_identity
+
+FLOPS = 2 * 2 * 2048 * 2048 * 512
+
+F32 = mybir.dt.float32
+BF16 = mybir.dt.bfloat16
+U32 = mybir.dt.uint32
+U8 = mybir.dt.uint8
+E4M3X4 = mybir.dt.float8_e4m3fn_x4
+E5M2X4 = mybir.dt.float8_e5m2_x4
+ADD = mybir.AluOpType.add
+MULT = mybir.AluOpType.mult
+COPY = mybir.ActivationFunctionType.Copy
+AX = mybir.AxisListType.X
+
+P = 128
+B, S, R, OUT, Q, NS, DO = 2, 1024, 512, 2048, 4, 4, 512
+G = 4
+RL = 16
+ST = 7
+HR = 4
+
+
+def tile_skilledlora_pb_v_kernel(tc, h, weights, lora_b, grad_out, out_0, out_1):
+    nc = tc.nc
+    with ExitStack() as ctx:
+        const = ctx.enter_context(tc.tile_pool(name="const", bufs=1))
+        big = ctx.enter_context(tc.tile_pool(name="big", bufs=1))
+        stage = ctx.enter_context(tc.tile_pool(name="stage", bufs=ST))
+        codes = ctx.enter_context(tc.tile_pool(name="codes", bufs=1))
+        psum = ctx.enter_context(tc.psum_pool(name="psum", bufs=2))
+        ctx.enter_context(tc.manual_schedule())
+
+        h_rows = h.rearrange("b s r -> (b s) r").rearrange("(g p j) r -> g p (j r)", p=P, j=4)
+        g_tok = grad_out.rearrange("b s w -> (b s) w").rearrange("(g p j) w -> g p j w", p=P, j=4)
+        o0_rows = out_0.rearrange("b s r -> (b s) r").rearrange("(g p j e) r -> g j p (e r)", p=P, j=2, e=2)
+
+        def codes_tile(width, nm):
+            c = codes.tile([P, width], U32, name=nm, align_bytes=64)
+            s = codes.tile([P, width], U8, name=nm + "_s", align_bytes=64)
+            return c, s
+
+        gt = [codes_tile(OUT, "gt%d" % g) for g in range(G)]
+        gf = [codes_tile(512, "gf%d" % f) for f in range(16)]
+        bm = [codes_tile(1024, "bm%d" % q) for q in range(Q)]
+        hc = [codes_tile(512, "hc%d" % g) for g in range(G)]
+
+        G_SLOT = (0, 1, 2, 3)
+        L_SLOT = (4, 0, 4, 0)
+        O_SLOT = (1, 2, 1, 2, 4, 3, 0, 1)
+
+        def big_tile(slot, dt):
+            if dt == F32:
+                t = big.tile([P, 4096], F32, name="big_f%d" % slot, tag="big%d" % slot, align_bytes=64)
+            else:
+                t = big.tile([P, 8192], BF16, name="big_b%d" % slot, tag="big%d" % slot, align_bytes=64)
+            return t
+
+        graw = {}
+        lraw = {}
+
+        def load_g(g):
+            graw[g] = big_tile(G_SLOT[g], BF16)
+            dst = graw[g][:].rearrange("p (j w) -> p j w", j=4)
+            cuts = [0, 512, 1024, 2048] if g == 0 else [0, 2048]
+            for a, z in zip(cuts[:-1], cuts[1:]):
+                nc.sync.dma_start(out=dst[:, :, a:z], in_=g_tok[g][:, :, a:z])
+
+        def load_l(q):
+            lraw[q] = big_tile(L_SLOT[q], BF16)
+            nc.sync.dma_start(out=lraw[q][:], in_=lora_b[q].rearrange("k (rh rl) d -> (k rh) (rl d)", rl=RL))
+
+        load_g(0)
+        w_bc = const.tile([P, 32], BF16, name="w_bc")
+        nc.sync.dma_start(out=w_bc[:], in_=weights.rearrange("b q k -> (b q k)").partition_broadcast(P))
+        load_g(1)
+        hraw = {}
+
+        def load_h(g):
+            hraw[g] = stage.tile([P, 2048], BF16, name="hr", tag="hr", bufs=HR, align_bytes=64)
+            nc.sync.dma_start(out=hraw[g][:], in_=h_rows[g])
+
+        for g in range(G):
+            load_h(g)
+        load_g(2)
+        load_g(3)
+        load_l(0)
+
+        ident = const.tile([P, P], F32, name="ident")
+        make_identity(nc, ident[:])
+        warm = const.tile([P, 1], F32, name="warm")
+        nc.scalar.activation(out=warm[:], in_=ident[:, 0:1], func=COPY, scale=2.0)
+        quad = const.tile([P, 4], F32, name="quad")
+        nc.vector.tensor_reduce(out=quad[:], in_=ident[:].rearrange("p (k r) -> p k r", k=4), axis=AX, op=ADD)
+        eye = const.tile([P, 32], F32, name="eye")
+        nc.vector.tensor_reduce(out=eye[:], in_=ident[:].rearrange("p (k r) -> p r k", k=4), axis=AX, op=ADD)
+        w1 = const.tile([P, 32], F32, name="w1")
+        nc.gpsimd.tensor_copy(out=w1[:], in_=w_bc[:])
+        w2 = const.tile([P, 32], F32, name="w2")
+        nc.gpsimd.tensor_scalar(out=w2[:], in0=w_bc[:], scalar1=2.0, scalar2=0.0, op0=MULT, op1=ADD)
+        parts = const.tile([P, 4, 8], F32, name="parts")
+        w1v = w1[:].rearrange("p (x k) -> p k x", k=4)
+        for k in range(NS):
+            nc.gpsimd.tensor_scalar(out=parts[:, k, :], in0=w1v[:, k, :], scalar1=quad[:, k : k + 1], scalar2=0.0, op0=MULT, op1=ADD)
+        half = const.tile([P, 2, 8], F32, name="half")
+        for i in range(2):
+            nc.gpsimd.tensor_tensor(out=half[:, i, :], in0=parts[:, 2 * i, :], in1=parts[:, 2 * i + 1, :], op=ADD)
+        wcol = const.tile([P, 8], F32, name="wcol")
+        nc.gpsimd.tensor_tensor(out=wcol[:], in0=half[:, 0, :], in1=half[:, 1, :], op=ADD)
+        wmix = const.tile([P, Q, B, 32], BF16, name="wmix")
+        for q in range(Q):
+            for b in range(B):
+                nc.gpsimd.tensor_scalar(out=wmix[:, q, b, :], in0=eye[:], scalar1=wcol[:, b * 4 + q : b * 4 + q + 1], scalar2=0.0, op0=MULT, op1=ADD)
+
+        wdup = const.tile([P, Q, B, 32, 2], BF16, name="wdup")
+        for j in range(2):
+            nc.gpsimd.tensor_copy(out=wdup[:, :, :, :, j].rearrange("p q b r -> p (q b r)"), in_=wmix[:].rearrange("p q b r -> p (q b r)"))
+
+        banks = {}
+        fst = {}
+
+        def bank_of(n):
+            g, r = divmod(n, 8)
+            f, x = divmod(r, 2)
+            return g, f, x, 2 * (f % 2) + x, f // 2
+
+        def transposes(n):
+            if n >= 32:
+                return
+            g, f, x, j, qp = bank_of(n)
+            bank = psum.tile([P, 512], F32, name="w_f", tag="w%d" % (n % 2), bufs=1)
+            banks[n] = bank
+            words = graw[g][:].bitcast(F32)
+            for qq in range(2):
+                for u in range(2):
+                    base = j * 1024 + (2 * qp + qq) * 256
+                    nc.tensor.transpose(bank[:, (2 * qq + u) * 128 : (2 * qq + u + 1) * 128], words[:, base + u : base + 256 : 2], ident[:])
+
+        def f_copy(n):
+            g, f, x, j, qp = bank_of(n)
+            if x == 0:
+                fst[g, f] = stage.tile([P, 2048], BF16, name="st", tag="st", align_bytes=64)
+            dst = fst[g, f][:].bitcast(F32)[:, x * 512 : (x + 1) * 512]
+            nc.scalar.copy(out=dst.rearrange("p (qq k u) -> p qq k u", qq=2, u=2), in_=banks.pop(n)[:].rearrange("p (qq u k) -> p qq k u", qq=2, u=2))
+
+        def quant(dst, cols, dtype, src):
+            c, s = dst
+            nc.vector.quantize_mx(out=c[:, cols].bitcast(dtype), scales=s[:, cols], in_=src)
+
+        def f_quant(i):
+            g, f = divmod(i, 4)
+            quant(gf[i], slice(0, 512), E5M2X4, fst.pop((g, f))[:])
+
+        tst = {}
+
+        def t_copy(g, q, eng):
+            st = stage.tile([P, 2048], BF16, name="st", tag="st", align_bytes=64)
+            tst[g, q] = st
+            src = graw[g][:].rearrange("p (t w) -> p t w", t=4)[:, :, q * 512 : (q + 1) * 512]
+            eng(out=st[:].rearrange("p (c i t) -> p c t i", i=4, t=4), in_=src.rearrange("p t (c i) -> p c t i", i=4))
+
+        def t_quant(g, q):
+            quant(gt[g], slice(q * 512, (q + 1) * 512), E5M2X4, tst.pop((g, q))[:])
+
+        hst = {}
+
+        def h_copy(g, eng):
+            st = stage.tile([P, 2048], BF16, name="st", tag="st", align_bytes=64)
+            hst[g] = st
+            src = hraw.pop(g)[:].rearrange("p (t r) -> p t r", t=4)
+            for rp in range(2):
+                eng(
+                    out=st[:, rp * 1024 : (rp + 1) * 1024].rearrange("p (e m t) -> p m t e", e=2, t=4),
+                    in_=src[:, :, rp * 256 : (rp + 1) * 256].rearrange("p t (m e) -> p m t e", e=2),
+                )
+
+        def h_quant(g):
+            quant(hc[g], slice(0, 512), E4M3X4, hst.pop(g)[:])
+
+        mbank = {}
+        mst = {}
+
+        def mix(m):
+            if m < 0 or m >= 16:
+                return
+            q, i = divmod(m, 4)
+            bank = psum.tile([P, 1024], BF16, name="w_b", tag="w%d" % (2 + m % 2), bufs=1)
+            mbank[m] = bank
+            view = bank[:].rearrange("p (b a r t) -> p b a r t", b=2, a=4, t=4)
+            for a in range(4):
+                for t in (1, 0, 3, 2):
+                    base = (4 * i + a) * 512
+                    odd = t % 2
+                    nc.tensor.matmul(
+                        view[:, :, a, :, t - 1 : t + 1] if odd else view[:, :, a, :, t],
+                        lhsT=lraw[q][:, base + t : base + 512 : 4],
+                        rhs=wdup[:, q].rearrange("p b r j -> p (b r j)") if odd else wmix[:, q].rearrange("p b r -> p (b r)"),
+                        start=True,
+                        stop=True,
+                    )
+
+        def m_copy(m, eng):
+            if m < 0 or m >= 16:
+                return
+            q, i = divmod(m, 4)
+            if i % 2 == 0:
+                mst[q, i // 2] = stage.tile([P, 2048], BF16, name="st", tag="st", align_bytes=64)
+            dst = mst[q, i // 2][:].rearrange("p (b i x) -> p b i x", b=2, i=2)[:, :, i % 2, :]
+            eng(out=dst, in_=mbank.pop(m)[:].rearrange("p (b x) -> p b x", b=2))
+
+        def m_quant(m):
+            if m < 0 or m >= 16:
+                return
+            q, i = divmod(m, 4)
+            src = mst.pop((q, i // 2))
+            for b in range(B):
+                start = b * 512 + (i // 2) * 256
+                quant(bm[q], slice(start, start + 256), E4M3X4, src[:, b * 1024 : (b + 1) * 1024])
+
+        xb = {}
+        yb = {}
+        ot = {}
+
+        def products(u):
+            if u >= 16:
+                return
+            q, rt = divmod(u, 4)
+            for b, d, tag in ((0, xb, "x"), (1, yb, "y")):
+                bank = psum.tile([P, 512], F32, name=tag, tag=tag, bufs=2)
+                d[u] = bank
+                for k in range(2):
+                    hcc, hcs = hc[2 * b + k]
+                    gtc, gts = gt[2 * b + k]
+                    ms = slice(rt * 128, (rt + 1) * 128)
+                    ns = slice(q * 512, (q + 1) * 512)
+                    nc.tensor.matmul_mx(
+                        out=bank[:],
+                        lhsT=hcc[:, ms].bitcast(E4M3X4),
+                        lhsT_scale=hcs[:, ms],
+                        rhs=gtc[:, ns].bitcast(E5M2X4),
+                        rhs_scale=gts[:, ns],
+                        start=(k == 0),
+                        stop=(k == 1),
+                    )
+
+        def shares_first(u):
+            q, rt = divmod(u, 4)
+            rp, e = divmod(rt, 2)
+            if e == 0:
+                ot[q, rp] = big_tile(O_SLOT[2 * q + rp], F32)
+            x = xb.pop(u)
+            for k in range(NS):
+                c = q * 4 + k
+                nc.scalar.activation(out=ot[q, rp][:, (2 * k + e) * 512 : (2 * k + e + 1) * 512], in_=x[:], func=COPY, scale=w2[:, c : c + 1])
+
+        def shares_second(u):
+            q, rt = divmod(u, 4)
+            rp, e = divmod(rt, 2)
+            y = yb.pop(u)
+            for k in range(NS):
+                c = 16 + q * 4 + k
+                o = ot[q, rp][:, (2 * k + e) * 512 : (2 * k + e + 1) * 512]
+                nc.vector.scalar_tensor_tensor(out=o, in0=y[:], scalar=w2[:, c : c + 1], in1=o, op0=MULT, op1=ADD)
+
+        def store_1(q, rp, ks):
+            dst = out_1[q, ks, rp * 256 : (rp + 1) * 256, :].rearrange("k (p e) d -> p k (e d)", e=2)
+            src = ot[q, rp][:].rearrange("p (k x) -> p k x", k=4)[:, ks, :]
+            nc.sync.dma_start(out=dst, in_=src)
+
+        zb = {}
+        zt = {}
+
+        def data_grad(n):
+            g, j = divmod(n, 4)
+            bank = psum.tile([P, 512], F32, name="w_f", tag="w%d" % (2 + n % 2), bufs=1)
+            zb[n] = bank
+            for q in range(Q):
+                fc, fs = gf[g * 4 + (q // 2) * 2 + j // 2]
+                ms = slice(((j % 2) * 2 + q % 2) * 128, ((j % 2) * 2 + q % 2 + 1) * 128)
+                ns = slice((g // 2) * 512, (g // 2 + 1) * 512)
+                nc.tensor.matmul_mx(
+                    out=bank[:],
+                    lhsT=fc[:, ms].bitcast(E5M2X4),
+                    lhsT_scale=fs[:, ms],
+                    rhs=bm[q][0][:, ns].bitcast(E4M3X4),
+                    rhs_scale=bm[q][1][:, ns],
+                    start=(q == 0),
+                    stop=(q == 3),
+                )
+
+        def data_out(n, on_scalar):
+            g, j = divmod(n, 4)
+            jp, e = divmod(j, 2)
+            first = (g, jp) not in zt
+            if first:
+                zt[g, jp] = stage.tile([P, 1024], F32, name="st_f", tag="st", align_bytes=64)
+            src = zb.pop(n)[:].rearrange("p (rl rh) -> p rh rl", rl=RL)
+            dst = zt[g, jp][:, e * 512 : (e + 1) * 512].rearrange("p (rh rl) -> p rh rl", rl=RL)
+            if on_scalar:
+                nc.scalar.activation(out=dst, in_=src, func=COPY, scale=2.0)
+            else:
+                nc.vector.tensor_scalar(out=dst, in0=src, scalar1=2.0, scalar2=None, op0=MULT)
+            if not first:
+                nc.sync.dma_start(out=o0_rows[g, jp], in_=zt.pop((g, jp))[:])
+
+        v_copy = nc.vector.tensor_copy
+        s_copy = nc.scalar.copy
+        T_AT = {0: [(0, 0)], 1: [(0, 1)], 2: [(0, 2)], 3: [(0, 3)], 4: [(1, 0)], 5: [(1, 1)], 6: [(1, 2)], 7: [(1, 3)], 8: [(2, 0), (2, 1)], 9: [(3, 0)], 10: [(2, 2)], 11: [(3, 1)], 12: [(2, 3)], 14: [(3, 2)], 17: [(3, 3)]}
+        F_AT = {0: 0, 1: 1, 2: 2, 3: 3, 4: 4, 5: 5, 6: 6, 7: 7, 8: 8, 9: 9, 10: 10, 11: 11, 13: 12, 15: 13, 16: 14, 18: 15}
+        H_AT = {4: [0], 5: [1], 6: [2], 7: [3]}
+        M_AT = {11: [0, 1], 12: [2, 3], 13: [4, 5], 14: [6, 7], 15: [8, 9], 16: [10, 11], 17: [12, 13], 18: [14, 15]}
+        O_AT = {20: [0, 1], 21: [2, 3], 22: [4, 5], 23: [6, 7], 24: [8, 9], 25: [10, 11], 26: [12, 13], 27: [14, 15]}
+        L_AT = {3: [(load_l, 1)], 11: [(load_l, 2)], 13: [(load_l, 3)]}
+        U0, LAST = 11, 27
+        S_TOK = {(0, 3), (1, 3)}
+        S_H = {0, 1, 2, 3}
+        S_OUT = {1, 3, 5, 7, 9, 11, 13, 15}
+        V_MC = set()
+        transposes(0)
+        transposes(1)
+        for b in range(LAST + 1):
+            u = b - U0
+            if b in F_AT:
+                f_copy(2 * F_AT[b])
+                f_copy(2 * F_AT[b] + 1)
+            for m in M_AT.get(b, ()):
+                m_copy(m, v_copy if m in V_MC else s_copy)
+            for n in O_AT.get(b, ()):
+                if n in S_OUT:
+                    data_out(n, True)
+            for x in H_AT.get(b, ()):
+                if x in S_H:
+                    h_copy(x, s_copy)
+            for gq in T_AT.get(b, ()):
+                if gq in S_TOK:
+                    t_copy(gq[0], gq[1], s_copy)
+            if 0 <= u < 16:
+                shares_first(u)
+            for gq in T_AT.get(b, ()):
+                if gq not in S_TOK:
+                    t_copy(gq[0], gq[1], v_copy)
+            for x in H_AT.get(b, ()):
+                if x not in S_H:
+                    h_copy(x, v_copy)
+            for gq in T_AT.get(b - 1, ()):
+                t_quant(*gq)
+            if b - 1 in F_AT:
+                f_quant(F_AT[b - 1])
+            for x in H_AT.get(b - 1, ()):
+                h_quant(x)
+            for m in M_AT.get(b - 1, ()):
+                if m % 2 == 1:
+                    m_quant(m)
+            for n in O_AT.get(b, ()):
+                if n not in S_OUT:
+                    data_out(n, False)
+            if 0 <= u < 16:
+                shares_second(u)
+            if b + 1 in F_AT and F_AT[b + 1] > 0:
+                transposes(2 * F_AT[b + 1])
+                transposes(2 * F_AT[b + 1] + 1)
+            if 0 <= u + 1 < 16:
+                products(u + 1)
+            for m in M_AT.get(b + 1, ()):
+                mix(m)
+            for l in L_AT.get(b, ()):
+                l[0](l[1])
+            if 0 <= u < 16:
+                q, rt = divmod(u, 4)
+                if rt % 2 == 1:
+                    store_1(q, rt // 2, slice(0, 2))
+                    store_1(q, rt // 2, slice(2, 4))
+            for n in O_AT.get(b + 1, ()):
+                data_grad(n)

@@ -20,8 +20,27 @@ P = 128
 B, S, R, OUT, Q, NS, DO = 2, 1024, 512, 2048, 4, 4, 512
 G = 4
 RL = 16
-ST = 7
-HR = 4
+G_SLOT = (0, 1, 3, 4)
+L_SLOT = (2, 0, 1, 0)
+O_SLOT = (2, 3, 2, 3, 1, 3, 2, 4)
+F_AT = [0, 1, 3, 2, 5, 4, 9, 6, 8, 7, 14, 13, 11, 40, 24, 29]
+T_AT = [0, 0, 2, 2, 5, 6, 3, 6, 7, 11, 13, 12, 8, 14, 24, 10]
+H_AT = [3, 5, 7, 5]
+M_AT = [7, 7, 9, 11, 13, 13, 17, 18, 14, 21, 25, 25, 28, 29, 35, 37]
+O_AT = [41, 43, 48, 47, 52, 55, 59, 61, 59, 65, 73, 69, 73, 71, 75, 76]
+U_AT = [12, 13, 15, 19, 22, 26, 27, 31, 33, 38, 45, 50, 53, 57, 63, 67]
+L_AT = {7: [("l", 1)], 11: [("l", 2)], 18: [("l", 3)]}
+F_ENG = ("SS", "SS", "SS", "VV", "SS", "SS", "SV", "VV", "VS", "SS", "SS", "SS", "VS", "SS", "SV", "VS")
+T_ENG = "VVSVVVSSVVSVVVSS"
+H_ENG = "VSSS"
+M_ENG = "SSSSSSSSSSVSSSSS"
+O_ENG = "VVVSVSVVSVSVSVSV"
+S_ORDER = "UMFOTH"
+V_ORDER = "OmftHThU"
+T_ORDER = "UOMF"
+O_WIDE = 0
+F_FIRST = 0
+LAST = 76
 
 
 def tile_skilledlora_pb_v_kernel(tc, h, weights, lora_b, grad_out, out_0, out_1):
@@ -29,9 +48,9 @@ def tile_skilledlora_pb_v_kernel(tc, h, weights, lora_b, grad_out, out_0, out_1)
     with ExitStack() as ctx:
         const = ctx.enter_context(tc.tile_pool(name="const", bufs=1))
         big = ctx.enter_context(tc.tile_pool(name="big", bufs=1))
-        stage = ctx.enter_context(tc.tile_pool(name="stage", bufs=ST))
+        stage = ctx.enter_context(tc.tile_pool(name="stage", bufs=1))
         codes = ctx.enter_context(tc.tile_pool(name="codes", bufs=1))
-        psum = ctx.enter_context(tc.psum_pool(name="psum", bufs=2))
+        psum = ctx.enter_context(tc.psum_pool(name="psum", bufs=1))
         ctx.enter_context(tc.manual_schedule())
 
         h_rows = h.rearrange("b s r -> (b s) r").rearrange("(g p j) r -> g p (j r)", p=P, j=4)
@@ -48,10 +67,6 @@ def tile_skilledlora_pb_v_kernel(tc, h, weights, lora_b, grad_out, out_0, out_1)
         bm = [codes_tile(1024, "bm%d" % q) for q in range(Q)]
         hc = [codes_tile(512, "hc%d" % g) for g in range(G)]
 
-        G_SLOT = (0, 1, 2, 3)
-        L_SLOT = (4, 0, 4, 0)
-        O_SLOT = (1, 2, 1, 2, 4, 3, 0, 1)
-
         def big_tile(slot, dt):
             if dt == F32:
                 t = big.tile([P, 4096], F32, name="big_f%d" % slot, tag="big%d" % slot, align_bytes=64)
@@ -59,8 +74,21 @@ def tile_skilledlora_pb_v_kernel(tc, h, weights, lora_b, grad_out, out_0, out_1)
                 t = big.tile([P, 8192], BF16, name="big_b%d" % slot, tag="big%d" % slot, align_bytes=64)
             return t
 
+        made = {}
+
+        def stage_tile(kind, depth, dt):
+            n = made.get(kind, 0)
+            made[kind] = n + 1
+            tag = "%s%d" % (kind, n % depth)
+            if dt == F32:
+                t = stage.tile([P, 1024], F32, name=tag + "_f", tag=tag, align_bytes=64)
+            else:
+                t = stage.tile([P, 2048], BF16, name=tag + "_b", tag=tag, align_bytes=64)
+            return t
+
         graw = {}
         lraw = {}
+        hraw = {}
 
         def load_g(g):
             graw[g] = big_tile(G_SLOT[g], BF16)
@@ -73,21 +101,23 @@ def tile_skilledlora_pb_v_kernel(tc, h, weights, lora_b, grad_out, out_0, out_1)
             lraw[q] = big_tile(L_SLOT[q], BF16)
             nc.sync.dma_start(out=lraw[q][:], in_=lora_b[q].rearrange("k (rh rl) d -> (k rh) (rl d)", rl=RL))
 
-        load_g(0)
+        def load_h(x):
+            for g in range(G):
+                hraw[g] = stage_tile("z", 4, BF16)
+                nc.sync.dma_start(out=hraw[g][:], in_=h_rows[g])
+
         w_bc = const.tile([P, 32], BF16, name="w_bc")
-        nc.sync.dma_start(out=w_bc[:], in_=weights.rearrange("b q k -> (b q k)").partition_broadcast(P))
+
+        def load_w(x):
+            nc.sync.dma_start(out=w_bc[:], in_=weights.rearrange("b q k -> (b q k)").partition_broadcast(P))
+
+        load_g(0)
+        load_w(0)
         load_g(1)
-        hraw = {}
-
-        def load_h(g):
-            hraw[g] = stage.tile([P, 2048], BF16, name="hr", tag="hr", bufs=HR, align_bytes=64)
-            nc.sync.dma_start(out=hraw[g][:], in_=h_rows[g])
-
-        for g in range(G):
-            load_h(g)
+        load_h(0)
+        load_l(0)
         load_g(2)
         load_g(3)
-        load_l(0)
 
         ident = const.tile([P, P], F32, name="ident")
         make_identity(nc, ident[:])
@@ -114,68 +144,65 @@ def tile_skilledlora_pb_v_kernel(tc, h, weights, lora_b, grad_out, out_0, out_1)
         for q in range(Q):
             for b in range(B):
                 nc.gpsimd.tensor_scalar(out=wmix[:, q, b, :], in0=eye[:], scalar1=wcol[:, b * 4 + q : b * 4 + q + 1], scalar2=0.0, op0=MULT, op1=ADD)
-
         wdup = const.tile([P, Q, B, 32, 2], BF16, name="wdup")
         for j in range(2):
             nc.gpsimd.tensor_copy(out=wdup[:, :, :, :, j].rearrange("p q b r -> p (q b r)"), in_=wmix[:].rearrange("p q b r -> p (q b r)"))
 
-        banks = {}
-        fst = {}
-
-        def bank_of(n):
-            g, r = divmod(n, 8)
-            f, x = divmod(r, 2)
-            return g, f, x, 2 * (f % 2) + x, f // 2
-
-        def transposes(n):
-            if n >= 32:
-                return
-            g, f, x, j, qp = bank_of(n)
-            bank = psum.tile([P, 512], F32, name="w_f", tag="w%d" % (n % 2), bufs=1)
-            banks[n] = bank
-            words = graw[g][:].bitcast(F32)
-            for qq in range(2):
-                for u in range(2):
-                    base = j * 1024 + (2 * qp + qq) * 256
-                    nc.tensor.transpose(bank[:, (2 * qq + u) * 128 : (2 * qq + u + 1) * 128], words[:, base + u : base + 256 : 2], ident[:])
-
-        def f_copy(n):
-            g, f, x, j, qp = bank_of(n)
-            if x == 0:
-                fst[g, f] = stage.tile([P, 2048], BF16, name="st", tag="st", align_bytes=64)
-            dst = fst[g, f][:].bitcast(F32)[:, x * 512 : (x + 1) * 512]
-            nc.scalar.copy(out=dst.rearrange("p (qq k u) -> p qq k u", qq=2, u=2), in_=banks.pop(n)[:].rearrange("p (qq u k) -> p qq k u", qq=2, u=2))
+        def copy_on(e, out, in_):
+            if e == "V":
+                nc.vector.tensor_copy(out=out, in_=in_)
+            elif e == "S":
+                nc.scalar.copy(out=out, in_=in_)
+            else:
+                nc.gpsimd.tensor_scalar(out=out, in0=in_, scalar1=1.0, scalar2=1.0, op0=MULT, op1=MULT)
 
         def quant(dst, cols, dtype, src):
             c, s = dst
             nc.vector.quantize_mx(out=c[:, cols].bitcast(dtype), scales=s[:, cols], in_=src)
 
-        def f_quant(i):
+        fbank = {}
+        fst = {}
+
+        def transposes(i):
             g, f = divmod(i, 4)
-            quant(gf[i], slice(0, 512), E5M2X4, fst.pop((g, f))[:])
+            words = graw[g][:].bitcast(F32)
+            for x in range(2):
+                j, qp = 2 * (f % 2) + x, f // 2
+                bank = psum.tile([P, 512], F32, name="w_f", tag="w%d" % x)
+                fbank[i, x] = bank
+                for qq in range(2):
+                    for u in range(2):
+                        base = j * 1024 + (2 * qp + qq) * 256
+                        nc.tensor.transpose(bank[:, (2 * qq + u) * 128 : (2 * qq + u + 1) * 128], words[:, base + u : base + 256 : 2], ident[:])
+
+        def f_copy(i):
+            fst[i] = stage_tile("f", 2, BF16)
+            for x in range(2):
+                dst = fst[i][:].bitcast(F32)[:, x * 512 : (x + 1) * 512]
+                copy_on(F_ENG[i][x], dst.rearrange("p (qq k u) -> p qq k u", qq=2, u=2), fbank.pop((i, x))[:].rearrange("p (qq u k) -> p qq k u", qq=2, u=2))
+
+        def f_quant(i):
+            quant(gf[i], slice(0, 512), E5M2X4, fst.pop(i)[:])
 
         tst = {}
 
-        def t_copy(g, q, eng):
-            st = stage.tile([P, 2048], BF16, name="st", tag="st", align_bytes=64)
-            tst[g, q] = st
+        def t_copy(n):
+            g, q = divmod(n, 4)
+            tst[n] = stage_tile("t", 3, BF16)
             src = graw[g][:].rearrange("p (t w) -> p t w", t=4)[:, :, q * 512 : (q + 1) * 512]
-            eng(out=st[:].rearrange("p (c i t) -> p c t i", i=4, t=4), in_=src.rearrange("p t (c i) -> p c t i", i=4))
+            copy_on(T_ENG[n], tst[n][:].rearrange("p (c i t) -> p c t i", i=4, t=4), src.rearrange("p t (c i) -> p c t i", i=4))
 
-        def t_quant(g, q):
-            quant(gt[g], slice(q * 512, (q + 1) * 512), E5M2X4, tst.pop((g, q))[:])
+        def t_quant(n):
+            g, q = divmod(n, 4)
+            quant(gt[g], slice(q * 512, (q + 1) * 512), E5M2X4, tst.pop(n)[:])
 
         hst = {}
 
-        def h_copy(g, eng):
-            st = stage.tile([P, 2048], BF16, name="st", tag="st", align_bytes=64)
+        def h_copy(g):
+            st = stage_tile("m", 2, BF16)
             hst[g] = st
             src = hraw.pop(g)[:].rearrange("p (t r) -> p t r", t=4)
-            for rp in range(2):
-                eng(
-                    out=st[:, rp * 1024 : (rp + 1) * 1024].rearrange("p (e m t) -> p m t e", e=2, t=4),
-                    in_=src[:, :, rp * 256 : (rp + 1) * 256].rearrange("p t (m e) -> p m t e", e=2),
-                )
+            copy_on(H_ENG[g], st[:].rearrange("p (r m t) -> p m t r", r=4, t=4), src.rearrange("p t (m r) -> p m t r", r=4))
 
         def h_quant(g):
             quant(hc[g], slice(0, 512), E4M3X4, hst.pop(g)[:])
@@ -184,10 +211,8 @@ def tile_skilledlora_pb_v_kernel(tc, h, weights, lora_b, grad_out, out_0, out_1)
         mst = {}
 
         def mix(m):
-            if m < 0 or m >= 16:
-                return
             q, i = divmod(m, 4)
-            bank = psum.tile([P, 1024], BF16, name="w_b", tag="w%d" % (2 + m % 2), bufs=1)
+            bank = psum.tile([P, 1024], BF16, name="w_b", tag="w%d" % (2 + m % 2))
             mbank[m] = bank
             view = bank[:].rearrange("p (b a r t) -> p b a r t", b=2, a=4, t=4)
             for a in range(4):
@@ -202,20 +227,18 @@ def tile_skilledlora_pb_v_kernel(tc, h, weights, lora_b, grad_out, out_0, out_1)
                         stop=True,
                     )
 
-        def m_copy(m, eng):
-            if m < 0 or m >= 16:
-                return
+        def m_copy(m):
             q, i = divmod(m, 4)
             if i % 2 == 0:
-                mst[q, i // 2] = stage.tile([P, 2048], BF16, name="st", tag="st", align_bytes=64)
-            dst = mst[q, i // 2][:].rearrange("p (b i x) -> p b i x", b=2, i=2)[:, :, i % 2, :]
-            eng(out=dst, in_=mbank.pop(m)[:].rearrange("p (b x) -> p b x", b=2))
+                mst[m // 2] = stage_tile("m", 2, BF16)
+            dst = mst[m // 2][:].rearrange("p (b i x) -> p b i x", b=2, i=2)[:, :, i % 2, :]
+            copy_on(M_ENG[m], dst, mbank.pop(m)[:].rearrange("p (b x) -> p b x", b=2))
 
         def m_quant(m):
-            if m < 0 or m >= 16:
+            if m % 2 == 0:
                 return
             q, i = divmod(m, 4)
-            src = mst.pop((q, i // 2))
+            src = mst.pop(m // 2)
             for b in range(B):
                 start = b * 512 + (i // 2) * 256
                 quant(bm[q], slice(start, start + 256), E4M3X4, src[:, b * 1024 : (b + 1) * 1024])
@@ -225,11 +248,9 @@ def tile_skilledlora_pb_v_kernel(tc, h, weights, lora_b, grad_out, out_0, out_1)
         ot = {}
 
         def products(u):
-            if u >= 16:
-                return
             q, rt = divmod(u, 4)
             for b, d, tag in ((0, xb, "x"), (1, yb, "y")):
-                bank = psum.tile([P, 512], F32, name=tag, tag=tag, bufs=2)
+                bank = psum.tile([P, 512], F32, name=tag, tag="%s%d" % (tag, u % 2))
                 d[u] = bank
                 for k in range(2):
                     hcc, hcs = hc[2 * b + k]
@@ -246,36 +267,39 @@ def tile_skilledlora_pb_v_kernel(tc, h, weights, lora_b, grad_out, out_0, out_1)
                         stop=(k == 1),
                     )
 
+        def o_part(u, k):
+            return ot[u // 2][:, (2 * k + u % 2) * 512 : (2 * k + u % 2 + 1) * 512]
+
         def shares_first(u):
-            q, rt = divmod(u, 4)
-            rp, e = divmod(rt, 2)
-            if e == 0:
-                ot[q, rp] = big_tile(O_SLOT[2 * q + rp], F32)
+            if u % 2 == 0:
+                ot[u // 2] = big_tile(O_SLOT[u // 2], F32)
             x = xb.pop(u)
             for k in range(NS):
-                c = q * 4 + k
-                nc.scalar.activation(out=ot[q, rp][:, (2 * k + e) * 512 : (2 * k + e + 1) * 512], in_=x[:], func=COPY, scale=w2[:, c : c + 1])
+                c = (u // 4) * 4 + k
+                nc.scalar.activation(out=o_part(u, k), in_=x[:], func=COPY, scale=w2[:, c : c + 1])
 
         def shares_second(u):
-            q, rt = divmod(u, 4)
-            rp, e = divmod(rt, 2)
             y = yb.pop(u)
             for k in range(NS):
-                c = 16 + q * 4 + k
-                o = ot[q, rp][:, (2 * k + e) * 512 : (2 * k + e + 1) * 512]
-                nc.vector.scalar_tensor_tensor(out=o, in0=y[:], scalar=w2[:, c : c + 1], in1=o, op0=MULT, op1=ADD)
+                c = 16 + (u // 4) * 4 + k
+                nc.vector.scalar_tensor_tensor(out=o_part(u, k), in0=y[:], scalar=w2[:, c : c + 1], in1=o_part(u, k), op0=MULT, op1=ADD)
 
-        def store_1(q, rp, ks):
-            dst = out_1[q, ks, rp * 256 : (rp + 1) * 256, :].rearrange("k (p e) d -> p k (e d)", e=2)
-            src = ot[q, rp][:].rearrange("p (k x) -> p k x", k=4)[:, ks, :]
-            nc.sync.dma_start(out=dst, in_=src)
+        def store_1(u):
+            if u % 2 == 0:
+                return
+            q, rp = divmod(u // 2, 2)
+            rows = out_1[q].rearrange("k (p x) d -> p k (x d)", p=P)
+            src = ot[u // 2][:].rearrange("p (k x) -> p k x", k=4)
+            for kp in range(2):
+                ks = slice(2 * kp, 2 * kp + 2)
+                nc.sync.dma_start(out=rows[:, ks, rp * 1024 : (rp + 1) * 1024], in_=src[:, ks, :])
 
         zb = {}
         zt = {}
 
         def data_grad(n):
             g, j = divmod(n, 4)
-            bank = psum.tile([P, 512], F32, name="w_f", tag="w%d" % (2 + n % 2), bufs=1)
+            bank = psum.tile([P, 512], F32, name="w_f", tag="w%d" % ((2 + n) % 4 if n >= O_WIDE else 2 + n % 2))
             zb[n] = bank
             for q in range(Q):
                 fc, fs = gf[g * 4 + (q // 2) * 2 + j // 2]
@@ -291,87 +315,109 @@ def tile_skilledlora_pb_v_kernel(tc, h, weights, lora_b, grad_out, out_0, out_1)
                     stop=(q == 3),
                 )
 
-        def data_out(n, on_scalar):
+        def data_out(n):
             g, j = divmod(n, 4)
             jp, e = divmod(j, 2)
             first = (g, jp) not in zt
             if first:
-                zt[g, jp] = stage.tile([P, 1024], F32, name="st_f", tag="st", align_bytes=64)
+                zt[g, jp] = stage_tile("z", 4, F32)
             src = zb.pop(n)[:].rearrange("p (rl rh) -> p rh rl", rl=RL)
             dst = zt[g, jp][:, e * 512 : (e + 1) * 512].rearrange("p (rh rl) -> p rh rl", rl=RL)
-            if on_scalar:
+            if O_ENG[n] == "S":
                 nc.scalar.activation(out=dst, in_=src, func=COPY, scale=2.0)
             else:
                 nc.vector.tensor_scalar(out=dst, in0=src, scalar1=2.0, scalar2=None, op0=MULT)
             if not first:
                 nc.sync.dma_start(out=o0_rows[g, jp], in_=zt.pop((g, jp))[:])
 
-        v_copy = nc.vector.tensor_copy
-        s_copy = nc.scalar.copy
-        T_AT = {0: [(0, 0)], 1: [(0, 1)], 2: [(0, 2)], 3: [(0, 3)], 4: [(1, 0)], 5: [(1, 1)], 6: [(1, 2)], 7: [(1, 3)], 8: [(2, 0), (2, 1)], 9: [(3, 0)], 10: [(2, 2)], 11: [(3, 1)], 12: [(2, 3)], 14: [(3, 2)], 17: [(3, 3)]}
-        F_AT = {0: 0, 1: 1, 2: 2, 3: 3, 4: 4, 5: 5, 6: 6, 7: 7, 8: 8, 9: 9, 10: 10, 11: 11, 13: 12, 15: 13, 16: 14, 18: 15}
-        H_AT = {4: [0], 5: [1], 6: [2], 7: [3]}
-        M_AT = {11: [0, 1], 12: [2, 3], 13: [4, 5], 14: [6, 7], 15: [8, 9], 16: [10, 11], 17: [12, 13], 18: [14, 15]}
-        O_AT = {20: [0, 1], 21: [2, 3], 22: [4, 5], 23: [6, 7], 24: [8, 9], 25: [10, 11], 26: [12, 13], 27: [14, 15]}
-        L_AT = {3: [(load_l, 1)], 11: [(load_l, 2)], 13: [(load_l, 3)]}
-        U0, LAST = 11, 27
-        S_TOK = {(0, 3), (1, 3)}
-        S_H = {0, 1, 2, 3}
-        S_OUT = {1, 3, 5, 7, 9, 11, 13, 15}
-        V_MC = set()
-        transposes(0)
-        transposes(1)
+        def at(table, b):
+            return [n for n in range(len(table)) if table[n] == b]
+
+        LOADERS = {"g": load_g, "l": load_l, "h": load_h}
+
+        def scalar_steps(b):
+            for ch in S_ORDER:
+                if ch == "F":
+                    for i in at(F_AT, b):
+                        f_copy(i)
+                if ch == "O":
+                    for n in at(O_AT, b):
+                        if O_ENG[n] == "S":
+                            data_out(n)
+                if ch == "H":
+                    for x in at(H_AT, b):
+                        if H_ENG[x] == "S":
+                            h_copy(x)
+                if ch == "T":
+                    for n in at(T_AT, b):
+                        if T_ENG[n] == "S":
+                            t_copy(n)
+                if ch == "U":
+                    for u in at(U_AT, b):
+                        shares_first(u)
+                if ch == "M":
+                    for m in at(M_AT, b):
+                        m_copy(m)
+            for n in at(T_AT, b):
+                if T_ENG[n] == "G":
+                    t_copy(n)
+
+        def vector_steps(b):
+            for ch in V_ORDER:
+                if ch == "T":
+                    for n in at(T_AT, b):
+                        if T_ENG[n] == "V":
+                            t_copy(n)
+                if ch == "H":
+                    for x in at(H_AT, b):
+                        if H_ENG[x] == "V":
+                            h_copy(x)
+                if ch == "t":
+                    for n in at(T_AT, b - 1):
+                        t_quant(n)
+                if ch == "f":
+                    for i in at(F_AT, b - 1):
+                        f_quant(i)
+                if ch == "h":
+                    for x in at(H_AT, b - 1):
+                        h_quant(x)
+                if ch == "m":
+                    for m in at(M_AT, b - 1):
+                        m_quant(m)
+                if ch == "O":
+                    for n in at(O_AT, b):
+                        if O_ENG[n] == "V":
+                            data_out(n)
+                if ch == "U":
+                    for u in at(U_AT, b):
+                        shares_second(u)
+
+        def tensor_steps(b):
+            for ch in T_ORDER:
+                if ch == "F":
+                    for i in at(F_AT, b + 1):
+                        if i != F_FIRST:
+                            transposes(i)
+                if ch == "U":
+                    for u in at(U_AT, b + 1):
+                        products(u)
+                if ch == "M":
+                    for m in at(M_AT, b + 1):
+                        mix(m)
+                if ch == "O":
+                    for n in at(O_AT, b + 1):
+                        data_grad(n)
+
+        transposes(F_FIRST)
         for b in range(LAST + 1):
-            u = b - U0
-            if b in F_AT:
-                f_copy(2 * F_AT[b])
-                f_copy(2 * F_AT[b] + 1)
-            for m in M_AT.get(b, ()):
-                m_copy(m, v_copy if m in V_MC else s_copy)
-            for n in O_AT.get(b, ()):
-                if n in S_OUT:
-                    data_out(n, True)
-            for x in H_AT.get(b, ()):
-                if x in S_H:
-                    h_copy(x, s_copy)
-            for gq in T_AT.get(b, ()):
-                if gq in S_TOK:
-                    t_copy(gq[0], gq[1], s_copy)
-            if 0 <= u < 16:
-                shares_first(u)
-            for gq in T_AT.get(b, ()):
-                if gq not in S_TOK:
-                    t_copy(gq[0], gq[1], v_copy)
-            for x in H_AT.get(b, ()):
-                if x not in S_H:
-                    h_copy(x, v_copy)
-            for gq in T_AT.get(b - 1, ()):
-                t_quant(*gq)
-            if b - 1 in F_AT:
-                f_quant(F_AT[b - 1])
-            for x in H_AT.get(b - 1, ()):
-                h_quant(x)
-            for m in M_AT.get(b - 1, ()):
-                if m % 2 == 1:
-                    m_quant(m)
-            for n in O_AT.get(b, ()):
-                if n not in S_OUT:
-                    data_out(n, False)
-            if 0 <= u < 16:
-                shares_second(u)
-            if b + 1 in F_AT and F_AT[b + 1] > 0:
-                transposes(2 * F_AT[b + 1])
-                transposes(2 * F_AT[b + 1] + 1)
-            if 0 <= u + 1 < 16:
-                products(u + 1)
-            for m in M_AT.get(b + 1, ()):
-                mix(m)
-            for l in L_AT.get(b, ()):
-                l[0](l[1])
-            if 0 <= u < 16:
-                q, rt = divmod(u, 4)
-                if rt % 2 == 1:
-                    store_1(q, rt // 2, slice(0, 2))
-                    store_1(q, rt // 2, slice(2, 4))
-            for n in O_AT.get(b + 1, ()):
-                data_grad(n)
+            scalar_steps(b)
+            vector_steps(b)
+            for kind, n in L_AT.get(b, ()):
+                if kind != "l":
+                    LOADERS[kind](n)
+            tensor_steps(b)
+            for kind, n in L_AT.get(b, ()):
+                if kind == "l":
+                    LOADERS[kind](n)
+            for u in at(U_AT, b):
+                store_1(u)

@@ -20,27 +20,7 @@ P = 128
 B, S, R, OUT, Q, NS, DO = 2, 1024, 512, 2048, 4, 4, 512
 G = 4
 RL = 16
-G_SLOT = (0, 1, 3, 4)
-L_SLOT = (2, 0, 1, 0)
-O_SLOT = (2, 3, 2, 3, 1, 3, 2, 4)
-F_AT = [0, 1, 3, 2, 5, 4, 9, 6, 8, 7, 14, 13, 11, 40, 24, 29]
-T_AT = [0, 0, 2, 2, 5, 6, 3, 6, 7, 11, 13, 12, 8, 14, 24, 10]
-H_AT = [3, 5, 7, 5]
-M_AT = [7, 7, 9, 11, 13, 13, 17, 18, 14, 21, 25, 25, 28, 29, 35, 37]
-O_AT = [41, 43, 48, 47, 52, 55, 59, 61, 59, 65, 73, 69, 73, 71, 75, 76]
-U_AT = [12, 13, 15, 19, 22, 26, 27, 31, 33, 38, 45, 50, 53, 57, 63, 67]
-L_AT = {7: [("l", 1)], 11: [("l", 2)], 18: [("l", 3)]}
-F_ENG = ("SS", "SS", "SS", "VV", "SS", "SS", "SV", "VV", "VS", "SS", "SS", "SS", "VS", "SS", "SV", "VS")
-T_ENG = "VVSVVVSSVVSVVVSS"
-H_ENG = "VSSS"
-M_ENG = "SSSSSSSSSSVSSSSS"
-O_ENG = "VVVSVSVVSVSVSVSV"
-S_ORDER = "UMFOTH"
-V_ORDER = "OmftHThU"
-T_ORDER = "UOMF"
-O_WIDE = 0
-F_FIRST = 0
-LAST = 76
+SLOT = {"g0": 0, "g1": 1, "h": 2, "l0": 3, "st0": 0, "w0_1": 0, "st1": 1, "g2": 4, "w0_0": 1, "w1_0": 2, "sf0": 0, "w1_1": 3, "sf1": 1, "g3": 5, "w2_0": 0, "st3": 2, "w2_1": 1, "w3_1": 2, "st2": 0, "w3_0": 3, "sf2": 0, "sf3": 1, "l1": 0, "st4": 1, "w6_0": 0, "st6": 2, "w6_1": 1, "w5_1": 3, "st5": 0, "sf5": 0, "w7_1": 2, "sh3": 0, "w5_0": 3, "w7_0": 3, "sh1": 1, "sf6": 0, "m2": 0, "sh0": 0, "sf7": 1, "sh2": 1, "m1": 1, "st7": 1, "X1": 0, "sm1": 0, "l3": 2, "X0": 1, "m3": 2, "sm0": 1, "st9": 2, "st8": 0, "w8_1": 0, "w4_0": 3, "m0": 1, "st10": 1, "sf8": 0, "sf4": 1, "w4_1": 2, "l2": 3, "w9_1": 0, "o0": 1, "w11_1": 3, "w8_0": 1, "w9_0": 2, "st12": 0, "X2": 0, "Y0": 0, "Y1": 1, "sf9": 1, "X3": 1, "st11": 0, "m7": 0, "st14": 2, "m5": 2, "Y2": 0, "sm3": 0, "m4": 1, "sm2": 1, "st15": 1, "m6": 0, "m13": 2, "o1": 0, "m12": 1, "st13": 0, "Y3": 1, "X5": 0, "sm6": 1, "m9": 0, "m11": 2, "sm4": 0, "o2": 1, "X4": 1, "Y4": 0, "Y5": 1, "X6": 0, "m8": 0, "m10": 1, "sm5": 1, "sf11": 0, "Y6": 1, "X7": 1, "o3": 3, "w10_0": 0, "Y7": 0, "w10_1": 2, "w11_0": 3, "m14": 1, "sf10": 1, "Y9": 1, "X8": 0, "sm7": 0, "X9": 1, "m15": 0, "o4": 0, "Y8": 0, "w15_1": 1, "X11": 1, "w13_1": 3, "Y10": 1, "O3": 0, "X10": 0, "zt1": 2, "O0": 2, "o5": 4, "O2": 0, "Y11": 0, "X12": 0, "zt0": 0, "O1": 0, "O6": 2, "Y12": 1, "o6": 1, "X13": 1, "Y13": 0, "zt3": 1, "O4": 0, "O7": 2, "X14": 0, "Y14": 1, "zt2": 2, "O11": 2, "o7": 2, "O5": 0, "X15": 1, "Y15": 0, "sf13": 0, "O9": 0, "sf15": 1, "O8": 3, "zt4": 0, "O10": 1, "zt5": 1, "w15_0": 0, "w12_1": 2, "w13_0": 3, "w12_0": 1, "w14_0": 0, "sf12": 1, "w14_1": 3, "sf14": 0, "O14": 1, "O15": 2, "zt7": 2, "O13": 0, "O12": 3, "zt6": 0}
 
 
 def tile_skilledlora_pb_v_kernel(tc, h, weights, lora_b, grad_out, out_0, out_1):
@@ -74,12 +54,8 @@ def tile_skilledlora_pb_v_kernel(tc, h, weights, lora_b, grad_out, out_0, out_1)
                 t = big.tile([P, 8192], BF16, name="big_b%d" % slot, tag="big%d" % slot, align_bytes=64)
             return t
 
-        made = {}
-
-        def stage_tile(kind, depth, dt):
-            n = made.get(kind, 0)
-            made[kind] = n + 1
-            tag = "%s%d" % (kind, n % depth)
+        def stage_tile(kind, slot, dt):
+            tag = "%s%d" % (kind, slot)
             if dt == F32:
                 t = stage.tile([P, 1024], F32, name=tag + "_f", tag=tag, align_bytes=64)
             else:
@@ -90,35 +66,28 @@ def tile_skilledlora_pb_v_kernel(tc, h, weights, lora_b, grad_out, out_0, out_1)
         lraw = {}
         hraw = {}
 
-        def load_g(g):
-            graw[g] = big_tile(G_SLOT[g], BF16)
+        def load_g(g, a, z):
+            if a == 0:
+                graw[g] = big_tile(SLOT["g%d" % g], BF16)
             dst = graw[g][:].rearrange("p (j w) -> p j w", j=4)
-            cuts = [0, 512, 1024, 2048] if g == 0 else [0, 2048]
-            for a, z in zip(cuts[:-1], cuts[1:]):
-                nc.sync.dma_start(out=dst[:, :, a:z], in_=g_tok[g][:, :, a:z])
+            nc.sync.dma_start(out=dst[:, :, a:z], in_=g_tok[g][:, :, a:z])
 
         def load_l(q):
-            lraw[q] = big_tile(L_SLOT[q], BF16)
+            lraw[q] = big_tile(SLOT["l%d" % q], BF16)
             nc.sync.dma_start(out=lraw[q][:], in_=lora_b[q].rearrange("k (rh rl) d -> (k rh) (rl d)", rl=RL))
 
-        def load_h(x):
-            for g in range(G):
-                hraw[g] = stage_tile("z", 4, BF16)
-                nc.sync.dma_start(out=hraw[g][:], in_=h_rows[g])
+        def load_h(g):
+            if "h" not in hraw:
+                hraw["h"] = big_tile(SLOT["h"], BF16)
+            nc.sync.dma_start(out=hraw["h"][:, g * 2048 : (g + 1) * 2048], in_=h_rows[g])
 
-        w_bc = const.tile([P, 32], BF16, name="w_bc")
+        wrow = const.tile([P, 32], BF16, name="wrow")
+        nc.vector.memset(wrow[:], 0.0)
+        ones = const.tile([P, P], BF16, name="ones")
+        nc.vector.memset(ones[:], 1.0)
 
-        def load_w(x):
-            nc.sync.dma_start(out=w_bc[:], in_=weights.rearrange("b q k -> (b q k)").partition_broadcast(P))
-
-        load_g(0)
-        load_w(0)
-        load_g(1)
-        load_h(0)
-        load_l(0)
-        load_g(2)
-        load_g(3)
-
+        load_g(0, 0, 512)
+        nc.sync.dma_start(out=wrow[0:1, :], in_=weights.rearrange("(o b) q k -> o (b q k)", o=1))
         ident = const.tile([P, P], F32, name="ident")
         make_identity(nc, ident[:])
         warm = const.tile([P, 1], F32, name="warm")
@@ -127,10 +96,12 @@ def tile_skilledlora_pb_v_kernel(tc, h, weights, lora_b, grad_out, out_0, out_1)
         nc.vector.tensor_reduce(out=quad[:], in_=ident[:].rearrange("p (k r) -> p k r", k=4), axis=AX, op=ADD)
         eye = const.tile([P, 32], F32, name="eye")
         nc.vector.tensor_reduce(out=eye[:], in_=ident[:].rearrange("p (k r) -> p r k", k=4), axis=AX, op=ADD)
+        wps = psum.tile([P, 512], F32, name="x", tag="x0")
+        nc.tensor.matmul(wps[:, 0:32], lhsT=ones[:], rhs=wrow[:], start=True, stop=True)
         w1 = const.tile([P, 32], F32, name="w1")
-        nc.gpsimd.tensor_copy(out=w1[:], in_=w_bc[:])
+        nc.scalar.copy(out=w1[:], in_=wps[:, 0:32])
         w2 = const.tile([P, 32], F32, name="w2")
-        nc.gpsimd.tensor_scalar(out=w2[:], in0=w_bc[:], scalar1=2.0, scalar2=0.0, op0=MULT, op1=ADD)
+        nc.scalar.activation(out=w2[:], in_=wps[:, 0:32], func=COPY, scale=2.0)
         parts = const.tile([P, 4, 8], F32, name="parts")
         w1v = w1[:].rearrange("p (x k) -> p k x", k=4)
         for k in range(NS):
@@ -163,34 +134,33 @@ def tile_skilledlora_pb_v_kernel(tc, h, weights, lora_b, grad_out, out_0, out_1)
         fbank = {}
         fst = {}
 
-        def transposes(i):
+        def transposes(i, x):
             g, f = divmod(i, 4)
             words = graw[g][:].bitcast(F32)
-            for x in range(2):
-                j, qp = 2 * (f % 2) + x, f // 2
-                bank = psum.tile([P, 512], F32, name="w_f", tag="w%d" % x)
-                fbank[i, x] = bank
-                for qq in range(2):
-                    for u in range(2):
-                        base = j * 1024 + (2 * qp + qq) * 256
-                        nc.tensor.transpose(bank[:, (2 * qq + u) * 128 : (2 * qq + u + 1) * 128], words[:, base + u : base + 256 : 2], ident[:])
+            j, qp = 2 * (f % 2) + x, f // 2
+            bank = psum.tile([P, 512], F32, name="w_f", tag="w%d" % SLOT["w%d_%d" % (i, x)])
+            fbank[i, x] = bank
+            for qq in range(2):
+                for u in range(2):
+                    base = j * 1024 + (2 * qp + qq) * 256
+                    nc.tensor.transpose(bank[:, (2 * qq + u) * 128 : (2 * qq + u + 1) * 128], words[:, base + u : base + 256 : 2], ident[:])
 
-        def f_copy(i):
-            fst[i] = stage_tile("f", 2, BF16)
-            for x in range(2):
-                dst = fst[i][:].bitcast(F32)[:, x * 512 : (x + 1) * 512]
-                copy_on(F_ENG[i][x], dst.rearrange("p (qq k u) -> p qq k u", qq=2, u=2), fbank.pop((i, x))[:].rearrange("p (qq u k) -> p qq k u", qq=2, u=2))
+        def f_copy(i, x, eng):
+            if i not in fst:
+                fst[i] = stage_tile("f", SLOT["sf%d" % i], BF16)
+            dst = fst[i][:].bitcast(F32)[:, x * 512 : (x + 1) * 512]
+            copy_on(eng, dst.rearrange("p (qq k u) -> p qq k u", qq=2, u=2), fbank.pop((i, x))[:].rearrange("p (qq u k) -> p qq k u", qq=2, u=2))
 
         def f_quant(i):
             quant(gf[i], slice(0, 512), E5M2X4, fst.pop(i)[:])
 
         tst = {}
 
-        def t_copy(n):
+        def t_copy(n, eng):
             g, q = divmod(n, 4)
-            tst[n] = stage_tile("t", 3, BF16)
+            tst[n] = stage_tile("t", SLOT["st%d" % n], BF16)
             src = graw[g][:].rearrange("p (t w) -> p t w", t=4)[:, :, q * 512 : (q + 1) * 512]
-            copy_on(T_ENG[n], tst[n][:].rearrange("p (c i t) -> p c t i", i=4, t=4), src.rearrange("p t (c i) -> p c t i", i=4))
+            copy_on(eng, tst[n][:].rearrange("p (c i t) -> p c t i", i=4, t=4), src.rearrange("p t (c i) -> p c t i", i=4))
 
         def t_quant(n):
             g, q = divmod(n, 4)
@@ -198,11 +168,11 @@ def tile_skilledlora_pb_v_kernel(tc, h, weights, lora_b, grad_out, out_0, out_1)
 
         hst = {}
 
-        def h_copy(g):
-            st = stage_tile("m", 2, BF16)
+        def h_copy(g, eng):
+            st = stage_tile("m", SLOT["sh%d" % g], BF16)
             hst[g] = st
-            src = hraw.pop(g)[:].rearrange("p (t r) -> p t r", t=4)
-            copy_on(H_ENG[g], st[:].rearrange("p (r m t) -> p m t r", r=4, t=4), src.rearrange("p t (m r) -> p m t r", r=4))
+            src = hraw["h"][:, g * 2048 : (g + 1) * 2048].rearrange("p (t r) -> p t r", t=4)
+            copy_on(eng, st[:].rearrange("p (r m t) -> p m t r", r=4, t=4), src.rearrange("p t (m r) -> p m t r", r=4))
 
         def h_quant(g):
             quant(hc[g], slice(0, 512), E4M3X4, hst.pop(g)[:])
@@ -212,7 +182,7 @@ def tile_skilledlora_pb_v_kernel(tc, h, weights, lora_b, grad_out, out_0, out_1)
 
         def mix(m):
             q, i = divmod(m, 4)
-            bank = psum.tile([P, 1024], BF16, name="w_b", tag="w%d" % (2 + m % 2))
+            bank = psum.tile([P, 1024], BF16, name="w_b", tag="w%d" % SLOT["m%d" % m])
             mbank[m] = bank
             view = bank[:].rearrange("p (b a r t) -> p b a r t", b=2, a=4, t=4)
             for a in range(4):
@@ -227,30 +197,28 @@ def tile_skilledlora_pb_v_kernel(tc, h, weights, lora_b, grad_out, out_0, out_1)
                         stop=True,
                     )
 
-        def m_copy(m):
+        def m_copy(m, eng):
             q, i = divmod(m, 4)
-            if i % 2 == 0:
-                mst[m // 2] = stage_tile("m", 2, BF16)
+            if m // 2 not in mst:
+                mst[m // 2] = stage_tile("m", SLOT["sm%d" % (m // 2)], BF16)
             dst = mst[m // 2][:].rearrange("p (b i x) -> p b i x", b=2, i=2)[:, :, i % 2, :]
-            copy_on(M_ENG[m], dst, mbank.pop(m)[:].rearrange("p (b x) -> p b x", b=2))
+            copy_on(eng, dst, mbank.pop(m)[:].rearrange("p (b x) -> p b x", b=2))
 
-        def m_quant(m):
-            if m % 2 == 0:
-                return
-            q, i = divmod(m, 4)
-            src = mst.pop(m // 2)
+        def m_quant(hm):
+            q, i = divmod(hm, 2)
+            src = mst.pop(hm)
             for b in range(B):
-                start = b * 512 + (i // 2) * 256
+                start = b * 512 + i * 256
                 quant(bm[q], slice(start, start + 256), E4M3X4, src[:, b * 1024 : (b + 1) * 1024])
 
         xb = {}
         yb = {}
         ot = {}
 
-        def products(u):
+        def products(u, b):
             q, rt = divmod(u, 4)
-            for b, d, tag in ((0, xb, "x"), (1, yb, "y")):
-                bank = psum.tile([P, 512], F32, name=tag, tag="%s%d" % (tag, u % 2))
+            for d, tag in (((xb, "x"), (yb, "y"))[b],):
+                bank = psum.tile([P, 512], F32, name=tag, tag="%s%d" % (tag, SLOT["%s%d" % (tag.replace("x", "X").replace("y", "Y"), u)]))
                 d[u] = bank
                 for k in range(2):
                     hcc, hcs = hc[2 * b + k]
@@ -271,8 +239,8 @@ def tile_skilledlora_pb_v_kernel(tc, h, weights, lora_b, grad_out, out_0, out_1)
             return ot[u // 2][:, (2 * k + u % 2) * 512 : (2 * k + u % 2 + 1) * 512]
 
         def shares_first(u):
-            if u % 2 == 0:
-                ot[u // 2] = big_tile(O_SLOT[u // 2], F32)
+            if u // 2 not in ot:
+                ot[u // 2] = big_tile(SLOT["o%d" % (u // 2)], F32)
             x = xb.pop(u)
             for k in range(NS):
                 c = (u // 4) * 4 + k
@@ -284,22 +252,19 @@ def tile_skilledlora_pb_v_kernel(tc, h, weights, lora_b, grad_out, out_0, out_1)
                 c = 16 + (u // 4) * 4 + k
                 nc.vector.scalar_tensor_tensor(out=o_part(u, k), in0=y[:], scalar=w2[:, c : c + 1], in1=o_part(u, k), op0=MULT, op1=ADD)
 
-        def store_1(u):
-            if u % 2 == 0:
-                return
-            q, rp = divmod(u // 2, 2)
+        def store_1(r, kp):
+            q, rp = divmod(r, 2)
             rows = out_1[q].rearrange("k (p x) d -> p k (x d)", p=P)
-            src = ot[u // 2][:].rearrange("p (k x) -> p k x", k=4)
-            for kp in range(2):
-                ks = slice(2 * kp, 2 * kp + 2)
-                nc.sync.dma_start(out=rows[:, ks, rp * 1024 : (rp + 1) * 1024], in_=src[:, ks, :])
+            src = ot[r][:].rearrange("p (k x) -> p k x", k=4)
+            ks = slice(2 * kp, 2 * kp + 2)
+            nc.sync.dma_start(out=rows[:, ks, rp * 1024 : (rp + 1) * 1024], in_=src[:, ks, :])
 
         zb = {}
         zt = {}
 
         def data_grad(n):
             g, j = divmod(n, 4)
-            bank = psum.tile([P, 512], F32, name="w_f", tag="w%d" % ((2 + n) % 4 if n >= O_WIDE else 2 + n % 2))
+            bank = psum.tile([P, 512], F32, name="w_f", tag="w%d" % SLOT["O%d" % n])
             zb[n] = bank
             for q in range(Q):
                 fc, fs = gf[g * 4 + (q // 2) * 2 + j // 2]
@@ -315,109 +280,311 @@ def tile_skilledlora_pb_v_kernel(tc, h, weights, lora_b, grad_out, out_0, out_1)
                     stop=(q == 3),
                 )
 
-        def data_out(n):
+        def data_out(n, eng):
             g, j = divmod(n, 4)
             jp, e = divmod(j, 2)
-            first = (g, jp) not in zt
-            if first:
-                zt[g, jp] = stage_tile("z", 4, F32)
+            if (g, jp) not in zt:
+                zt[g, jp] = stage_tile("t", SLOT["zt%d" % (n // 2)], F32)
             src = zb.pop(n)[:].rearrange("p (rl rh) -> p rh rl", rl=RL)
             dst = zt[g, jp][:, e * 512 : (e + 1) * 512].rearrange("p (rh rl) -> p rh rl", rl=RL)
-            if O_ENG[n] == "S":
+            if eng == "S":
                 nc.scalar.activation(out=dst, in_=src, func=COPY, scale=2.0)
             else:
                 nc.vector.tensor_scalar(out=dst, in0=src, scalar1=2.0, scalar2=None, op0=MULT)
-            if not first:
-                nc.sync.dma_start(out=o0_rows[g, jp], in_=zt.pop((g, jp))[:])
 
-        def at(table, b):
-            return [n for n in range(len(table)) if table[n] == b]
+        def store_0(p):
+            nc.sync.dma_start(out=o0_rows[p // 2, p % 2], in_=zt.pop((p // 2, p % 2))[:])
 
-        LOADERS = {"g": load_g, "l": load_l, "h": load_h}
-
-        def scalar_steps(b):
-            for ch in S_ORDER:
-                if ch == "F":
-                    for i in at(F_AT, b):
-                        f_copy(i)
-                if ch == "O":
-                    for n in at(O_AT, b):
-                        if O_ENG[n] == "S":
-                            data_out(n)
-                if ch == "H":
-                    for x in at(H_AT, b):
-                        if H_ENG[x] == "S":
-                            h_copy(x)
-                if ch == "T":
-                    for n in at(T_AT, b):
-                        if T_ENG[n] == "S":
-                            t_copy(n)
-                if ch == "U":
-                    for u in at(U_AT, b):
-                        shares_first(u)
-                if ch == "M":
-                    for m in at(M_AT, b):
-                        m_copy(m)
-            for n in at(T_AT, b):
-                if T_ENG[n] == "G":
-                    t_copy(n)
-
-        def vector_steps(b):
-            for ch in V_ORDER:
-                if ch == "T":
-                    for n in at(T_AT, b):
-                        if T_ENG[n] == "V":
-                            t_copy(n)
-                if ch == "H":
-                    for x in at(H_AT, b):
-                        if H_ENG[x] == "V":
-                            h_copy(x)
-                if ch == "t":
-                    for n in at(T_AT, b - 1):
-                        t_quant(n)
-                if ch == "f":
-                    for i in at(F_AT, b - 1):
-                        f_quant(i)
-                if ch == "h":
-                    for x in at(H_AT, b - 1):
-                        h_quant(x)
-                if ch == "m":
-                    for m in at(M_AT, b - 1):
-                        m_quant(m)
-                if ch == "O":
-                    for n in at(O_AT, b):
-                        if O_ENG[n] == "V":
-                            data_out(n)
-                if ch == "U":
-                    for u in at(U_AT, b):
-                        shares_second(u)
-
-        def tensor_steps(b):
-            for ch in T_ORDER:
-                if ch == "F":
-                    for i in at(F_AT, b + 1):
-                        if i != F_FIRST:
-                            transposes(i)
-                if ch == "U":
-                    for u in at(U_AT, b + 1):
-                        products(u)
-                if ch == "M":
-                    for m in at(M_AT, b + 1):
-                        mix(m)
-                if ch == "O":
-                    for n in at(O_AT, b + 1):
-                        data_grad(n)
-
-        transposes(F_FIRST)
-        for b in range(LAST + 1):
-            scalar_steps(b)
-            vector_steps(b)
-            for kind, n in L_AT.get(b, ()):
-                if kind != "l":
-                    LOADERS[kind](n)
-            tensor_steps(b)
-            for kind, n in L_AT.get(b, ()):
-                if kind == "l":
-                    LOADERS[kind](n)
-            for u in at(U_AT, b):
-                store_1(u)
+        load_g(0, 512, 1024)
+        load_g(0, 1024, 2048)
+        load_g(1, 0, 2048)
+        load_h(3)
+        load_h(1)
+        load_l(0)
+        load_h(0)
+        t_copy(0, "S")
+        load_h(2)
+        transposes(0, 1)
+        t_copy(1, "V")
+        load_g(2, 0, 2048)
+        transposes(0, 0)
+        transposes(1, 0)
+        f_copy(0, 1, "S")
+        t_quant(0)
+        transposes(1, 1)
+        f_copy(0, 0, "S")
+        t_quant(1)
+        f_copy(1, 0, "S")
+        f_quant(0)
+        load_g(3, 0, 2048)
+        transposes(2, 0)
+        t_copy(3, "S")
+        transposes(2, 1)
+        f_copy(1, 1, "V")
+        transposes(3, 1)
+        t_copy(2, "V")
+        transposes(3, 0)
+        f_quant(1)
+        f_copy(2, 0, "S")
+        t_quant(3)
+        f_copy(2, 1, "S")
+        t_quant(2)
+        f_copy(3, 0, "S")
+        f_quant(2)
+        load_l(1)
+        t_copy(4, "S")
+        transposes(6, 0)
+        t_copy(6, "V")
+        transposes(6, 1)
+        transposes(5, 1)
+        f_copy(3, 1, "V")
+        t_copy(5, "G")
+        f_copy(5, 1, "V")
+        transposes(7, 1)
+        h_copy(3, "S")
+        transposes(5, 0)
+        f_copy(5, 0, "V")
+        transposes(7, 0)
+        t_quant(4)
+        f_quant(5)
+        h_copy(1, "S")
+        f_quant(3)
+        h_quant(3)
+        t_quant(6)
+        t_quant(5)
+        f_copy(6, 0, "S")
+        h_quant(1)
+        f_copy(6, 1, "S")
+        mix(2)
+        h_copy(0, "V")
+        f_copy(7, 1, "S")
+        h_copy(2, "S")
+        f_quant(6)
+        mix(1)
+        h_quant(0)
+        t_copy(7, "V")
+        products(1, 0)
+        m_copy(2, "S")
+        load_l(3)
+        products(0, 0)
+        h_quant(2)
+        f_copy(7, 0, "S")
+        mix(3)
+        t_quant(7)
+        m_copy(1, "S")
+        f_quant(7)
+        t_copy(9, "S")
+        t_copy(8, "V")
+        transposes(8, 1)
+        transposes(4, 0)
+        mix(0)
+        m_copy(3, "V")
+        t_copy(10, "G")
+        f_copy(8, 1, "V")
+        f_copy(4, 0, "S")
+        transposes(4, 1)
+        load_l(2)
+        m_copy(0, "V")
+        transposes(9, 1)
+        shares_first(1)
+        f_copy(4, 1, "V")
+        transposes(11, 1)
+        t_quant(8)
+        transposes(8, 0)
+        transposes(9, 0)
+        t_copy(12, "V")
+        shares_first(0)
+        f_quant(4)
+        products(2, 0)
+        t_quant(12)
+        t_quant(9)
+        products(0, 1)
+        m_quant(1)
+        products(1, 1)
+        f_copy(9, 1, "S")
+        products(3, 0)
+        t_copy(11, "G")
+        shares_second(0)
+        f_copy(9, 0, "S")
+        mix(7)
+        f_copy(8, 0, "S")
+        t_copy(14, "S")
+        mix(5)
+        shares_second(1)
+        store_1(0, 0)
+        products(2, 1)
+        m_copy(7, "S")
+        mix(4)
+        m_quant(0)
+        store_1(0, 1)
+        t_quant(10)
+        m_copy(5, "S")
+        f_quant(8)
+        t_copy(15, "S")
+        mix(6)
+        m_copy(4, "V")
+        t_quant(11)
+        mix(13)
+        m_quant(2)
+        f_quant(9)
+        shares_first(2)
+        t_quant(14)
+        mix(12)
+        t_copy(13, "G")
+        shares_second(2)
+        products(3, 1)
+        m_copy(6, "S")
+        products(5, 0)
+        shares_first(3)
+        m_copy(13, "V")
+        mix(9)
+        m_quant(3)
+        shares_second(3)
+        mix(11)
+        m_copy(9, "S")
+        store_1(1, 0)
+        shares_first(5)
+        t_quant(13)
+        products(4, 0)
+        store_1(1, 1)
+        m_copy(12, "V")
+        products(4, 1)
+        t_quant(15)
+        products(5, 1)
+        shares_first(4)
+        m_quant(6)
+        products(6, 0)
+        shares_second(5)
+        mix(8)
+        mix(10)
+        m_copy(8, "S")
+        shares_second(4)
+        m_copy(11, "S")
+        f_copy(11, 1, "S")
+        products(6, 1)
+        store_1(2, 0)
+        m_copy(10, "S")
+        products(7, 0)
+        shares_first(6)
+        transposes(10, 0)
+        m_quant(4)
+        store_1(2, 1)
+        products(7, 1)
+        shares_second(6)
+        transposes(10, 1)
+        transposes(11, 0)
+        shares_first(7)
+        mix(14)
+        f_copy(10, 0, "V")
+        shares_second(7)
+        products(9, 1)
+        products(8, 0)
+        m_copy(14, "S")
+        store_1(3, 0)
+        products(9, 0)
+        f_copy(11, 0, "S")
+        mix(15)
+        shares_first(9)
+        f_quant(11)
+        store_1(3, 1)
+        m_quant(5)
+        shares_second(9)
+        products(8, 1)
+        transposes(15, 1)
+        m_copy(15, "S")
+        products(11, 0)
+        shares_first(8)
+        transposes(13, 1)
+        m_quant(7)
+        products(10, 1)
+        shares_second(8)
+        data_grad(3)
+        store_1(4, 0)
+        f_copy(10, 1, "S")
+        products(10, 0)
+        data_out(3, "S")
+        data_grad(0)
+        f_quant(10)
+        store_1(4, 1)
+        shares_first(10)
+        data_grad(2)
+        shares_second(10)
+        products(11, 1)
+        data_out(2, "S")
+        products(12, 0)
+        shares_first(11)
+        data_out(0, "V")
+        store_0(1)
+        data_grad(1)
+        shares_second(11)
+        data_grad(6)
+        store_1(5, 0)
+        products(12, 1)
+        shares_first(12)
+        products(13, 0)
+        data_out(1, "V")
+        store_1(5, 1)
+        products(13, 1)
+        data_out(6, "V")
+        store_0(0)
+        data_grad(4)
+        shares_second(12)
+        shares_first(13)
+        data_grad(7)
+        products(14, 0)
+        data_out(7, "V")
+        products(14, 1)
+        data_out(4, "V")
+        store_0(3)
+        data_grad(11)
+        shares_first(14)
+        shares_second(13)
+        data_grad(5)
+        store_1(6, 0)
+        products(15, 0)
+        data_out(5, "S")
+        shares_second(14)
+        store_1(6, 1)
+        products(15, 1)
+        f_copy(13, 1, "S")
+        store_0(2)
+        data_grad(9)
+        f_copy(15, 1, "S")
+        shares_first(15)
+        data_grad(8)
+        data_out(9, "V")
+        data_grad(10)
+        data_out(11, "V")
+        shares_second(15)
+        data_out(8, "S")
+        transposes(15, 0)
+        transposes(12, 1)
+        data_out(10, "S")
+        store_1(7, 0)
+        store_0(4)
+        transposes(13, 0)
+        f_copy(15, 0, "S")
+        store_0(5)
+        transposes(12, 0)
+        store_1(7, 1)
+        f_quant(15)
+        f_copy(13, 0, "S")
+        transposes(14, 0)
+        f_copy(12, 0, "S")
+        f_quant(13)
+        transposes(14, 1)
+        f_copy(12, 1, "V")
+        f_copy(14, 0, "S")
+        data_grad(14)
+        f_copy(14, 1, "V")
+        f_quant(12)
+        data_grad(15)
+        data_out(14, "S")
+        f_quant(14)
+        data_grad(13)
+        data_out(15, "V")
+        store_0(7)
+        data_grad(12)
+        data_out(13, "S")
+        data_out(12, "V")
+        store_0(6)

from contextlib import ExitStack

import concourse.mybir as mybir
from concourse.masks import make_identity

FLOPS = 2 * 2 * 2048 * 2048 * 512

F32 = mybir.dt.float32
BF16 = mybir.dt.bfloat16
U32 = mybir.dt.uint32
U8 = mybir.dt.uint8
E4M3X4 = mybir.dt.float8_e4m3fn_x4
E5M2X4 = mybir.dt.float8_e5m2_x4
ADD = mybir.AluOpType.add
MULT = mybir.AluOpType.mult
COPY = mybir.ActivationFunctionType.Copy
AX = mybir.AxisListType.X

P = 128
B, S, R, OUT, Q, NS, DO = 2, 1024, 512, 2048, 4, 4, 512
G = 4
RL = 16
SLOT = {"g0": 0, "g1": 1, "h": 2, "l0": 3, "st0": 0, "w0_1": 0, "st1": 1, "g2": 4, "w0_0": 1, "w1_0": 2, "sf0": 0, "w1_1": 3, "sf1": 1, "g3": 5, "w2_0": 0, "st3": 2, "w2_1": 1, "w3_1": 2, "st2": 0, "w3_0": 3, "sf2": 0, "sf3": 1, "l1": 0, "st4": 1, "w6_0": 0, "st6": 2, "w6_1": 1, "w5_1": 3, "st5": 0, "sf5": 0, "w7_1": 2, "sh3": 0, "w5_0": 3, "w7_0": 3, "sh1": 1, "sf6": 0, "m2": 0, "sh0": 0, "sf7": 1, "sh2": 1, "m1": 1, "st7": 1, "X1": 0, "sm1": 0, "l3": 2, "X0": 1, "m3": 2, "sm0": 1, "st9": 2, "st8": 0, "w8_1": 0, "w4_0": 3, "m0": 1, "st10": 1, "sf8": 0, "sf4": 1, "w4_1": 2, "l2": 3, "w9_1": 0, "o0": 1, "w11_1": 3, "w8_0": 1, "w9_0": 2, "st12": 0, "X2": 0, "Y0": 0, "Y1": 1, "sf9": 1, "X3": 1, "st11": 0, "m7": 0, "st14": 2, "m5": 2, "Y2": 0, "sm3": 0, "m4": 1, "sm2": 1, "st15": 1, "m6": 0, "m13": 2, "o1": 0, "m12": 1, "st13": 0, "Y3": 1, "X5": 0, "sm6": 1, "m9": 0, "m11": 2, "sm4": 0, "o2": 1, "X4": 1, "Y4": 0, "Y5": 1, "X6": 0, "m8": 0, "m10": 1, "sm5": 1, "sf11": 0, "Y6": 1, "X7": 1, "o3": 3, "w10_0": 0, "Y7": 0, "w10_1": 2, "w11_0": 3, "m14": 1, "sf10": 1, "Y9": 1, "X8": 0, "sm7": 0, "X9": 1, "m15": 0, "o4": 0, "Y8": 0, "w15_1": 1, "X11": 1, "w13_1": 3, "Y10": 1, "O3": 0, "X10": 0, "zt1": 2, "O0": 2, "o5": 4, "O2": 0, "Y11": 0, "X12": 0, "zt0": 0, "O1": 0, "O6": 2, "Y12": 1, "o6": 1, "X13": 1, "Y13": 0, "zt3": 1, "O4": 0, "O7": 2, "X14": 0, "Y14": 1, "zt2": 2, "O11": 2, "o7": 2, "O5": 0, "X15": 1, "Y15": 0, "sf13": 0, "O9": 0, "sf15": 1, "O8": 3, "zt4": 0, "O10": 1, "zt5": 1, "w15_0": 0, "w12_1": 2, "w13_0": 3, "w12_0": 1, "w14_0": 0, "sf12": 1, "w14_1": 3, "sf14": 0, "O14": 1, "O15": 2, "zt7": 2, "O13": 0, "O12": 3, "zt6": 0}


def tile_skilledlora_pb_v_kernel(tc, h, weights, lora_b, grad_out, out_0, out_1):
    nc = tc.nc
    with ExitStack() as ctx:
        const = ctx.enter_context(tc.tile_pool(name="const", bufs=1))
        big = ctx.enter_context(tc.tile_pool(name="big", bufs=1))
        stage = ctx.enter_context(tc.tile_pool(name="stage", bufs=1))
        codes = ctx.enter_context(tc.tile_pool(name="codes", bufs=1))
        psum = ctx.enter_context(tc.psum_pool(name="psum", bufs=1))
        ctx.enter_context(tc.manual_schedule())

        h_rows = h.rearrange("b s r -> (b s) r").rearrange("(g p j) r -> g p (j r)", p=P, j=4)
        g_tok = grad_out.rearrange("b s w -> (b s) w").rearrange("(g p j) w -> g p j w", p=P, j=4)
        o0_rows = out_0.rearrange("b s r -> (b s) r").rearrange("(g p j e) r -> g j p (e r)", p=P, j=2, e=2)

        def codes_tile(width, nm):
            c = codes.tile([P, width], U32, name=nm, align_bytes=64)
            s = codes.tile([P, width], U8, name=nm + "_s", align_bytes=64)
            return c, s

        gt = [codes_tile(OUT, "gt%d" % g) for g in range(G)]
        gf = [codes_tile(512, "gf%d" % f) for f in range(16)]
        bm = [codes_tile(1024, "bm%d" % q) for q in range(Q)]
        hc = [codes_tile(512, "hc%d" % g) for g in range(G)]

        def big_tile(slot, dt):
            if dt == F32:
                t = big.tile([P, 4096], F32, name="big_f%d" % slot, tag="big%d" % slot, align_bytes=64)
            else:
                t = big.tile([P, 8192], BF16, name="big_b%d" % slot, tag="big%d" % slot, align_bytes=64)
            return t

        def stage_tile(kind, slot, dt):
            tag = "%s%d" % (kind, slot)
            if dt == F32:
                t = stage.tile([P, 1024], F32, name=tag + "_f", tag=tag, align_bytes=64)
            else:
                t = stage.tile([P, 2048], BF16, name=tag + "_b", tag=tag, align_bytes=64)
            return t

        graw = {}
        lraw = {}
        hraw = {}

        def load_g(g, a, z):
            if a == 0:
                graw[g] = big_tile(SLOT["g%d" % g], BF16)
            dst = graw[g][:].rearrange("p (j w) -> p j w", j=4)
            nc.sync.dma_start(out=dst[:, :, a:z], in_=g_tok[g][:, :, a:z])

        def load_l(q):
            lraw[q] = big_tile(SLOT["l%d" % q], BF16)
            nc.sync.dma_start(out=lraw[q][:], in_=lora_b[q].rearrange("k (rh rl) d -> (k rh) (rl d)", rl=RL))

        def load_h(g):
            if "h" not in hraw:
                hraw["h"] = big_tile(SLOT["h"], BF16)
            nc.sync.dma_start(out=hraw["h"][:, g * 2048 : (g + 1) * 2048], in_=h_rows[g])

        wrow = const.tile([P, 32], BF16, name="wrow")
        nc.vector.memset(wrow[:], 0.0)
        ones = const.tile([P, P], BF16, name="ones")
        nc.vector.memset(ones[:], 1.0)

        load_g(0, 0, 512)
        nc.sync.dma_start(out=wrow[0:1, :], in_=weights.rearrange("(o b) q k -> o (b q k)", o=1))
        ident = const.tile([P, P], F32, name="ident")
        make_identity(nc, ident[:])
        warm = const.tile([P, 1], F32, name="warm")
        nc.scalar.activation(out=warm[:], in_=ident[:, 0:1], func=COPY, scale=2.0)
        quad = const.tile([P, 4], F32, name="quad")
        nc.vector.tensor_reduce(out=quad[:], in_=ident[:].rearrange("p (k r) -> p k r", k=4), axis=AX, op=ADD)
        eye = const.tile([P, 32], F32, name="eye")
        nc.vector.tensor_reduce(out=eye[:], in_=ident[:].rearrange("p (k r) -> p r k", k=4), axis=AX, op=ADD)
        wps = psum.tile([P, 512], F32, name="x", tag="x0")
        nc.tensor.matmul(wps[:, 0:32], lhsT=ones[:], rhs=wrow[:], start=True, stop=True)
        w1 = const.tile([P, 32], F32, name="w1")
        nc.scalar.copy(out=w1[:], in_=wps[:, 0:32])
        w2 = const.tile([P, 32], F32, name="w2")
        nc.scalar.activation(out=w2[:], in_=wps[:, 0:32], func=COPY, scale=2.0)
        parts = const.tile([P, 4, 8], F32, name="parts")
        w1v = w1[:].rearrange("p (x k) -> p k x", k=4)
        for k in range(NS):
            nc.gpsimd.tensor_scalar(out=parts[:, k, :], in0=w1v[:, k, :], scalar1=quad[:, k : k + 1], scalar2=0.0, op0=MULT, op1=ADD)
        half = const.tile([P, 2, 8], F32, name="half")
        for i in range(2):
            nc.gpsimd.tensor_tensor(out=half[:, i, :], in0=parts[:, 2 * i, :], in1=parts[:, 2 * i + 1, :], op=ADD)
        wcol = const.tile([P, 8], F32, name="wcol")
        nc.gpsimd.tensor_tensor(out=wcol[:], in0=half[:, 0, :], in1=half[:, 1, :], op=ADD)
        wmix = const.tile([P, Q, B, 32], BF16, name="wmix")
        for q in range(Q):
            for b in range(B):
                nc.gpsimd.tensor_scalar(out=wmix[:, q, b, :], in0=eye[:], scalar1=wcol[:, b * 4 + q : b * 4 + q + 1], scalar2=0.0, op0=MULT, op1=ADD)
        wdup = const.tile([P, Q, B, 32, 2], BF16, name="wdup")
        for j in range(2):
            nc.gpsimd.tensor_copy(out=wdup[:, :, :, :, j].rearrange("p q b r -> p (q b r)"), in_=wmix[:].rearrange("p q b r -> p (q b r)"))

        def copy_on(e, out, in_):
            if e == "V":
                nc.vector.tensor_copy(out=out, in_=in_)
            elif e == "S":
                nc.scalar.copy(out=out, in_=in_)
            else:
                nc.gpsimd.tensor_scalar(out=out, in0=in_, scalar1=1.0, scalar2=1.0, op0=MULT, op1=MULT)

        def quant(dst, cols, dtype, src):
            c, s = dst
            nc.vector.quantize_mx(out=c[:, cols].bitcast(dtype), scales=s[:, cols], in_=src)

        fbank = {}
        fst = {}

        def transposes(i, x):
            g, f = divmod(i, 4)
            words = graw[g][:].bitcast(F32)
            j, qp = 2 * (f % 2) + x, f // 2
            bank = psum.tile([P, 512], F32, name="w_f", tag="w%d" % SLOT["w%d_%d" % (i, x)])
            fbank[i, x] = bank
            for qq in range(2):
                for u in range(2):
                    base = j * 1024 + (2 * qp + qq) * 256
                    nc.tensor.transpose(bank[:, (2 * qq + u) * 128 : (2 * qq + u + 1) * 128], words[:, base + u : base + 256 : 2], ident[:])

        def f_copy(i, x, eng):
            if i not in fst:
                fst[i] = stage_tile("f", SLOT["sf%d" % i], BF16)
            dst = fst[i][:].bitcast(F32)[:, x * 512 : (x + 1) * 512]
            copy_on(eng, dst.rearrange("p (qq k u) -> p qq k u", qq=2, u=2), fbank.pop((i, x))[:].rearrange("p (qq u k) -> p qq k u", qq=2, u=2))

        def f_quant(i):
            quant(gf[i], slice(0, 512), E5M2X4, fst.pop(i)[:])

        tst = {}

        def t_copy(n, eng):
            g, q = divmod(n, 4)
            tst[n] = stage_tile("t", SLOT["st%d" % n], BF16)
            src = graw[g][:].rearrange("p (t w) -> p t w", t=4)[:, :, q * 512 : (q + 1) * 512]
            copy_on(eng, tst[n][:].rearrange("p (c i t) -> p c t i", i=4, t=4), src.rearrange("p t (c i) -> p c t i", i=4))

        def t_quant(n):
            g, q = divmod(n, 4)
            quant(gt[g], slice(q * 512, (q + 1) * 512), E5M2X4, tst.pop(n)[:])

        hst = {}

        def h_copy(g, eng):
            st = stage_tile("m", SLOT["sh%d" % g], BF16)
            hst[g] = st
            src = hraw["h"][:, g * 2048 : (g + 1) * 2048].rearrange("p (t r) -> p t r", t=4)
            copy_on(eng, st[:].rearrange("p (r m t) -> p m t r", r=4, t=4), src.rearrange("p t (m r) -> p m t r", r=4))

        def h_quant(g):
            quant(hc[g], slice(0, 512), E4M3X4, hst.pop(g)[:])

        mbank = {}
        mst = {}

        def mix(m):
            q, i = divmod(m, 4)
            bank = psum.tile([P, 1024], BF16, name="w_b", tag="w%d" % SLOT["m%d" % m])
            mbank[m] = bank
            view = bank[:].rearrange("p (b a r t) -> p b a r t", b=2, a=4, t=4)
            for a in range(4):
                for t in (1, 0, 3, 2):
                    base = (4 * i + a) * 512
                    odd = t % 2
                    nc.tensor.matmul(
                        view[:, :, a, :, t - 1 : t + 1] if odd else view[:, :, a, :, t],
                        lhsT=lraw[q][:, base + t : base + 512 : 4],
                        rhs=wdup[:, q].rearrange("p b r j -> p (b r j)") if odd else wmix[:, q].rearrange("p b r -> p (b r)"),
                        start=True,
                        stop=True,
                    )

        def m_copy(m, eng):
            q, i = divmod(m, 4)
            if m // 2 not in mst:
                mst[m // 2] = stage_tile("m", SLOT["sm%d" % (m // 2)], BF16)
            dst = mst[m // 2][:].rearrange("p (b i x) -> p b i x", b=2, i=2)[:, :, i % 2, :]
            copy_on(eng, dst, mbank.pop(m)[:].rearrange("p (b x) -> p b x", b=2))

        def m_quant(hm):
            q, i = divmod(hm, 2)
            src = mst.pop(hm)
            for b in range(B):
                start = b * 512 + i * 256
                quant(bm[q], slice(start, start + 256), E4M3X4, src[:, b * 1024 : (b + 1) * 1024])

        xb = {}
        yb = {}
        ot = {}

        def products(u, b):
            q, rt = divmod(u, 4)
            for d, tag in (((xb, "x"), (yb, "y"))[b],):
                bank = psum.tile([P, 512], F32, name=tag, tag="%s%d" % (tag, SLOT["%s%d" % (tag.replace("x", "X").replace("y", "Y"), u)]))
                d[u] = bank
                for k in range(2):
                    hcc, hcs = hc[2 * b + k]
                    gtc, gts = gt[2 * b + k]
                    ms = slice(rt * 128, (rt + 1) * 128)
                    ns = slice(q * 512, (q + 1) * 512)
                    nc.tensor.matmul_mx(
                        out=bank[:],
                        lhsT=hcc[:, ms].bitcast(E4M3X4),
                        lhsT_scale=hcs[:, ms],
                        rhs=gtc[:, ns].bitcast(E5M2X4),
                        rhs_scale=gts[:, ns],
                        start=(k == 0),
                        stop=(k == 1),
                    )

        def o_part(u, k):
            return ot[u // 2][:, (2 * k + u % 2) * 512 : (2 * k + u % 2 + 1) * 512]

        def shares_first(u):
            if u // 2 not in ot:
                ot[u // 2] = big_tile(SLOT["o%d" % (u // 2)], F32)
            x = xb.pop(u)
            for k in range(NS):
                c = (u // 4) * 4 + k
                nc.scalar.activation(out=o_part(u, k), in_=x[:], func=COPY, scale=w2[:, c : c + 1])

        def shares_second(u):
            y = yb.pop(u)
            for k in range(NS):
                c = 16 + (u // 4) * 4 + k
                nc.vector.scalar_tensor_tensor(out=o_part(u, k), in0=y[:], scalar=w2[:, c : c + 1], in1=o_part(u, k), op0=MULT, op1=ADD)

        def store_1(r, kp):
            q, rp = divmod(r, 2)
            rows = out_1[q].rearrange("k (p x) d -> p k (x d)", p=P)
            src = ot[r][:].rearrange("p (k x) -> p k x", k=4)
            ks = slice(2 * kp, 2 * kp + 2)
            nc.sync.dma_start(out=rows[:, ks, rp * 1024 : (rp + 1) * 1024], in_=src[:, ks, :])

        zb = {}
        zt = {}

        def data_grad(n):
            g, j = divmod(n, 4)
            bank = psum.tile([P, 512], F32, name="w_f", tag="w%d" % SLOT["O%d" % n])
            zb[n] = bank
            for q in range(Q):
                fc, fs = gf[g * 4 + (q // 2) * 2 + j // 2]
                ms = slice(((j % 2) * 2 + q % 2) * 128, ((j % 2) * 2 + q % 2 + 1) * 128)
                ns = slice((g // 2) * 512, (g // 2 + 1) * 512)
                nc.tensor.matmul_mx(
                    out=bank[:],
                    lhsT=fc[:, ms].bitcast(E5M2X4),
                    lhsT_scale=fs[:, ms],
                    rhs=bm[q][0][:, ns].bitcast(E4M3X4),
                    rhs_scale=bm[q][1][:, ns],
                    start=(q == 0),
                    stop=(q == 3),
                )

        def data_out(n, eng):
            g, j = divmod(n, 4)
            jp, e = divmod(j, 2)
            if (g, jp) not in zt:
                zt[g, jp] = stage_tile("t", SLOT["zt%d" % (n // 2)], F32)
            src = zb.pop(n)[:].rearrange("p (rl rh) -> p rh rl", rl=RL)
            dst = zt[g, jp][:, e * 512 : (e + 1) * 512].rearrange("p (rh rl) -> p rh rl", rl=RL)
            if eng == "S":
                nc.scalar.activation(out=dst, in_=src, func=COPY, scale=2.0)
            else:
                nc.vector.tensor_scalar(out=dst, in0=src, scalar1=2.0, scalar2=None, op0=MULT)

        def store_0(p):
            nc.sync.dma_start(out=o0_rows[p // 2, p % 2], in_=zt.pop((p // 2, p % 2))[:])

        load_g(0, 512, 1024)
        load_g(0, 1024, 2048)
        load_g(1, 0, 2048)
        load_h(3)
        load_h(1)
        load_l(0)
        load_h(0)
        t_copy(0, "S")
        load_h(2)
        transposes(0, 1)
        t_copy(1, "V")
        load_g(2, 0, 2048)
        transposes(0, 0)
        transposes(1, 0)
        f_copy(0, 1, "S")
        t_quant(0)
        transposes(1, 1)
        f_copy(0, 0, "S")
        t_quant(1)
        f_copy(1, 0, "S")
        f_quant(0)
        load_g(3, 0, 2048)
        transposes(2, 0)
        t_copy(3, "S")
        transposes(2, 1)
        f_copy(1, 1, "V")
        transposes(3, 1)
        t_copy(2, "V")
        transposes(3, 0)
        f_quant(1)
        f_copy(2, 0, "S")
        t_quant(3)
        f_copy(2, 1, "S")
        t_quant(2)
        f_copy(3, 0, "S")
        f_quant(2)
        load_l(1)
        t_copy(4, "S")
        transposes(6, 0)
        t_copy(6, "V")
        transposes(6, 1)
        transposes(5, 1)
        f_copy(3, 1, "V")
        t_copy(5, "G")
        f_copy(5, 1, "V")
        transposes(7, 1)
        h_copy(3, "S")
        transposes(5, 0)
        f_copy(5, 0, "V")
        transposes(7, 0)
        t_quant(4)
        f_quant(5)
        h_copy(1, "S")
        f_quant(3)
        h_quant(3)
        t_quant(6)
        t_quant(5)
        f_copy(6, 0, "S")
        h_quant(1)
        f_copy(6, 1, "S")
        mix(2)
        h_copy(0, "V")
        f_copy(7, 1, "S")
        h_copy(2, "S")
        f_quant(6)
        mix(1)
        h_quant(0)
        t_copy(7, "V")
        products(1, 0)
        m_copy(2, "S")
        load_l(3)
        products(0, 0)
        h_quant(2)
        f_copy(7, 0, "S")
        mix(3)
        t_quant(7)
        m_copy(1, "S")
        f_quant(7)
        t_copy(9, "S")
        t_copy(8, "V")
        transposes(8, 1)
        transposes(4, 0)
        mix(0)
        m_copy(3, "V")
        t_copy(10, "G")
        f_copy(8, 1, "V")
        f_copy(4, 0, "S")
        transposes(4, 1)
        load_l(2)
        m_copy(0, "V")
        transposes(9, 1)
        shares_first(1)
        f_copy(4, 1, "V")
        transposes(11, 1)
        t_quant(8)
        transposes(8, 0)
        transposes(9, 0)
        t_copy(12, "V")
        shares_first(0)
        f_quant(4)
        products(2, 0)
        t_quant(12)
        t_quant(9)
        products(0, 1)
        m_quant(1)
        products(1, 1)
        f_copy(9, 1, "S")
        products(3, 0)
        t_copy(11, "G")
        shares_second(0)
        f_copy(9, 0, "S")
        mix(7)
        f_copy(8, 0, "S")
        t_copy(14, "S")
        mix(5)
        shares_second(1)
        store_1(0, 0)
        products(2, 1)
        m_copy(7, "S")
        mix(4)
        m_quant(0)
        store_1(0, 1)
        t_quant(10)
        m_copy(5, "S")
        f_quant(8)
        t_copy(15, "S")
        mix(6)
        m_copy(4, "V")
        t_quant(11)
        mix(13)
        m_quant(2)
        f_quant(9)
        shares_first(2)
        t_quant(14)
        mix(12)
        t_copy(13, "G")
        shares_second(2)
        products(3, 1)
        m_copy(6, "S")
        products(5, 0)
        shares_first(3)
        m_copy(13, "V")
        mix(9)
        m_quant(3)
        shares_second(3)
        mix(11)
        m_copy(9, "S")
        store_1(1, 0)
        shares_first(5)
        t_quant(13)
        products(4, 0)
        store_1(1, 1)
        m_copy(12, "V")
        products(4, 1)
        t_quant(15)
        products(5, 1)
        shares_first(4)
        m_quant(6)
        products(6, 0)
        shares_second(5)
        mix(8)
        mix(10)
        m_copy(8, "S")
        shares_second(4)
        m_copy(11, "S")
        f_copy(11, 1, "S")
        products(6, 1)
        store_1(2, 0)
        m_copy(10, "S")
        products(7, 0)
        shares_first(6)
        transposes(10, 0)
        m_quant(4)
        store_1(2, 1)
        products(7, 1)
        shares_second(6)
        transposes(10, 1)
        transposes(11, 0)
        shares_first(7)
        mix(14)
        f_copy(10, 0, "V")
        shares_second(7)
        products(9, 1)
        products(8, 0)
        m_copy(14, "S")
        store_1(3, 0)
        products(9, 0)
        f_copy(11, 0, "S")
        mix(15)
        shares_first(9)
        f_quant(11)
        store_1(3, 1)
        m_quant(5)
        shares_second(9)
        products(8, 1)
        transposes(15, 1)
        m_copy(15, "S")
        products(11, 0)
        shares_first(8)
        transposes(13, 1)
        m_quant(7)
        products(10, 1)
        shares_second(8)
        data_grad(3)
        store_1(4, 0)
        f_copy(10, 1, "S")
        products(10, 0)
        data_out(3, "S")
        data_grad(0)
        f_quant(10)
        store_1(4, 1)
        shares_first(10)
        data_grad(2)
        shares_second(10)
        products(11, 1)
        data_out(2, "S")
        products(12, 0)
        shares_first(11)
        data_out(0, "V")
        store_0(1)
        data_grad(1)
        shares_second(11)
        data_grad(6)
        store_1(5, 0)
        products(12, 1)
        shares_first(12)
        products(13, 0)
        data_out(1, "V")
        store_1(5, 1)
        products(13, 1)
        data_out(6, "V")
        store_0(0)
        data_grad(4)
        shares_second(12)
        shares_first(13)
        data_grad(7)
        products(14, 0)
        data_out(7, "V")
        products(14, 1)
        data_out(4, "V")
        store_0(3)
        data_grad(11)
        shares_first(14)
        shares_second(13)
        data_grad(5)
        store_1(6, 0)
        products(15, 0)
        data_out(5, "S")
        shares_second(14)
        store_1(6, 1)
        products(15, 1)
        f_copy(13, 1, "S")
        store_0(2)
        data_grad(9)
        f_copy(15, 1, "S")
        shares_first(15)
        data_grad(8)
        data_out(9, "V")
        data_grad(10)
        data_out(11, "V")
        shares_second(15)
        data_out(8, "S")
        transposes(15, 0)
        transposes(12, 1)
        data_out(10, "S")
        store_1(7, 0)
        store_0(4)
        transposes(13, 0)
        f_copy(15, 0, "S")
        store_0(5)
        transposes(12, 0)
        store_1(7, 1)
        f_quant(15)
        f_copy(13, 0, "S")
        transposes(14, 0)
        f_copy(12, 0, "S")
        f_quant(13)
        transposes(14, 1)
        f_copy(12, 1, "V")
        f_copy(14, 0, "S")
        data_grad(14)
        f_copy(14, 1, "V")
        f_quant(12)
        data_grad(15)
        data_out(14, "S")
        f_quant(14)
        data_grad(13)
        data_out(15, "V")
        store_0(7)
        data_grad(12)
        data_out(13, "S")
        data_out(12, "V")
        store_0(6)
